import numpy as np
import ml_dtypes


def mxq(x, axis, fmt="e4m3"):
    dtype, down = {"e4m3": (ml_dtypes.float8_e4m3fn, 7), "e5m2": (ml_dtypes.float8_e5m2, 14)}[fmt]
    v = np.moveaxis(np.asarray(x, np.float32).astype(ml_dtypes.bfloat16).astype(np.float64), axis, -1)
    blocks = v.reshape(v.shape[:-1] + (-1, 32))
    amax = np.abs(blocks).max(-1, keepdims=True)
    byte = np.maximum(np.where(amax > 0, np.frexp(amax)[1] - 1 + 127, 0) - down, 1)
    scale = np.exp2(byte - 127.0)
    codes = (blocks / scale).astype(np.float32).astype(dtype).astype(np.float64)
    return np.moveaxis((codes * scale).reshape(v.shape), -1, axis)


WIDE = False


def mx_kscale(k):
    if not WIDE:
        return np.ones(k)
    levels = np.array([10, -10, 5, -5, 0])
    a = np.random.permutation(np.resize(levels, k // 512 * 4)).reshape(k // 512, 4)
    idx = np.arange(k)
    return np.exp2(a[idx // 512, idx % 128 // 32])


BF16 = ml_dtypes.bfloat16


def bf(x):
    return np.asarray(x, np.float32).astype(BF16)


def f64(x):
    return np.asarray(x).astype(np.float64)


E2M1 = np.array([0.0, 0.5, 1.0, 1.5, 2.0, 3.0, 4.0, 6.0, -0.0, -0.5, -1.0, -1.5, -2.0, -3.0, -4.0, -6.0])


def pack_weight(w, fmt):
    k, n = w.shape
    w = f64(bf(w)).reshape(k // 32, 32, n)
    amax = np.abs(w).max(1)
    if fmt == "e4m3":
        byte = np.frexp(amax)[1] - 1 + 127 - 7
    else:
        mant, ex = np.frexp(amax / 6.0)
        byte = np.where(mant > 0.5, ex, ex - 1) + 127
    byte = np.clip(np.where(amax > 0, byte, 1), 1, 254)
    scaled = (w * np.exp2(127.0 - byte)[:, None, :]).reshape(k, n).astype(np.float32)
    by_word = np.ascontiguousarray(scaled.reshape(k // 512, 128, 4, n).transpose(0, 1, 3, 2))
    if fmt == "e4m3":
        words = by_word.astype(ml_dtypes.float8_e4m3fn).view(np.uint8)
    else:
        c = by_word.astype(ml_dtypes.float4_e2m1fn).view(np.uint8) & 0xF
        words = c[..., 0::2] | (c[..., 1::2] << 4)
    return np.ascontiguousarray(words), np.ascontiguousarray(byte.astype(np.uint8).reshape(k // 512, 16, n))


def unpack_weight(words, scales, fmt):
    g, p, n, _ = words.shape
    if fmt == "e4m3":
        vals = np.ascontiguousarray(words).view(ml_dtypes.float8_e4m3fn).astype(np.float64)
    else:
        nib = np.empty((g, p, n, 4), np.uint8)
        nib[..., 0::2] = words & 0xF
        nib[..., 1::2] = words >> 4
        vals = E2M1[nib]
    vals = vals * np.repeat(np.exp2(scales.astype(np.float64) - 127.0), 8, axis=1)[..., None]
    return vals.transpose(0, 1, 3, 2).reshape(g * 512, n)

def pack4(w):
    words, scales = pack_weight(w, "e2m1")
    return words.reshape(words.shape[0], 128, -1), scales


def unpack4(words, scales):
    return unpack_weight(words.reshape(words.shape[0], 128, -1, 2), scales, "e2m1")


B, L, S, D, DA, H, MLP = 2, 3, 256, 1024, 1024, 16, 4096
EPS = 1e-5


def layer_norm(u, g, b):
    mu = u.mean(-1, keepdims=True)
    var = ((u - mu) ** 2).mean(-1, keepdims=True)
    return (u - mu) / np.sqrt(var + EPS) * g + b


def setup_inputs():
    s = mx_kscale(DA)
    r = np.random.standard_normal
    h_attn = bf(r((B, S, DA)) * 2.0 * s)
    x = bf(r((B, S, D)))
    words, scales = pack4(r((DA, D)) * 0.5 / np.sqrt(DA) / s[:, None])
    return {"h_attn": h_attn, "x": x,
            "attn_out_W_words": words, "attn_out_W_scales": scales, "attn_out_b": bf(r(D) * 0.2),
            "attn_norm_g": bf(1.0 + 0.1 * r(D)), "attn_norm_b": bf(r(D) * 0.1)}


def reference(h_attn, x, attn_out_W_words, attn_out_W_scales, attn_out_b, attn_norm_g, attn_norm_b):
    o = (mxq(f64(h_attn), 2, "e4m3") @ unpack4(attn_out_W_words, attn_out_W_scales)) + f64(attn_out_b)
    return f64(x) + layer_norm(o, f64(attn_norm_g), f64(attn_norm_b))

@@ -1,0 +1,201 @@
+from contextlib import ExitStack
+
+import concourse.mybir as mybir
+from concourse.masks import make_identity
+
+F32 = mybir.dt.float32
+BF16 = mybir.dt.bfloat16
+I32 = mybir.dt.int32
+U32 = mybir.dt.uint32
+U8 = mybir.dt.uint8
+FP8X4 = mybir.dt.float8_e4m3fn_x4
+FP4X4 = mybir.dt.float4_e2m1fn_x4
+ALU = mybir.AluOpType
+ACT = mybir.ActivationFunctionType
+
+P = 128
+PACK = 4
+K_PASS = P * PACK
+TOKENS = 512
+K = 1024
+N = 1024
+BANK = 512
+TOKEN_TILES = TOKENS // P
+PASSES = K // K_PASS
+BANKS = N // BANK
+WORDS = K_PASS // 2
+EPS = 1e-5
+
+FLOPS = 2 * TOKENS * K * N
+
+
+def tile_dcadecoderblock_pb_kernel(
+    tc,
+    h_attn,
+    x,
+    attn_out_W_words,
+    attn_out_W_scales,
+    attn_out_b,
+    attn_norm_g,
+    attn_norm_b,
+    out,
+):
+    nc = tc.nc
+    h_tiles = h_attn.flatten_outer_dims().rearrange("(i p) k -> i p k", p=P)
+    x_tiles = x.flatten_outer_dims().rearrange("(i p) n -> i p n", p=P)
+    out_tiles = out.flatten_outer_dims().rearrange("(i p) n -> i p n", p=P)
+
+    with ExitStack() as ctx:
+        keep = ctx.enter_context(tc.tile_pool(name="keep", bufs=1))
+        rows = ctx.enter_context(tc.tile_pool(name="rows", bufs=TOKEN_TILES))
+        small = ctx.enter_context(tc.tile_pool(name="small", bufs=TOKEN_TILES))
+        psum_gain = ctx.enter_context(tc.psum_pool(name="psum_gain", bufs=1))
+        psum_stage = ctx.enter_context(tc.psum_pool(name="psum_stage", bufs=3))
+        psum_acc = ctx.enter_context(tc.psum_pool(name="psum_acc", bufs=4))
+
+        w_scales = keep.tile([P, PASSES, N], U8, align_bytes=64)
+        nc.vector.memset(w_scales[:].rearrange("p g n -> p (g n)").bitcast(I32), 0)
+        b_row = keep.tile([P, N], BF16)
+        shift_row = keep.tile([P, N], BF16)
+        gain_row = keep.tile([P, N], BF16)
+        ones = keep.tile([P, P], BF16)
+        eps = keep.tile([P, 1], F32)
+        nc.vector.memset(b_row[:], 0.0)
+        nc.vector.memset(shift_row[:], 0.0)
+        nc.vector.memset(gain_row[:], 0.0)
+        nc.vector.memset(ones[:], 1.0)
+        nc.vector.memset(eps[:], EPS)
+        identity = keep.tile([P, P], F32)
+        make_identity(nc, identity[:])
+        table_warm = keep.tile([P, 1], F32)
+        nc.scalar.activation(out=table_warm[:], in_=eps[:], func=ACT.Sqrt)
+
+        h_sb = []
+        x_sb = []
+        for i in range(TOKEN_TILES):
+            h_sb.append(rows.tile([P, K], BF16, name="h_sb"))
+            x_sb.append(rows.tile([P, N], BF16, name="x_sb"))
+        w_words = keep.tile([P, PASSES, 2 * N], U8, align_bytes=64)
+
+        nc.sync.dma_start(out=h_sb[0][:], in_=h_tiles[0])
+        for q in range(4):
+            nc.sync.dma_start(
+                out=w_scales[32 * q : 32 * q + 4, :, :].bitcast(I32),
+                in_=attn_out_W_scales[:, 4 * q : 4 * q + 4, :].rearrange("g r n -> r g n").bitcast(I32),
+            )
+        nc.scalar.dma_start(out=b_row[0:1, :], in_=attn_out_b.unsqueeze(0))
+        nc.scalar.dma_start(out=shift_row[0:1, :], in_=attn_norm_b.unsqueeze(0))
+        nc.sync.dma_start(
+            out=w_words[:].bitcast(I32),
+            in_=attn_out_W_words.rearrange("g p b -> p g b").bitcast(I32),
+        )
+        nc.scalar.dma_start(out=gain_row[0:1, :], in_=attn_norm_g.unsqueeze(0))
+        nc.sync.dma_start(out=x_sb[0][:], in_=x_tiles[0])
+        for i in range(1, TOKEN_TILES):
+            nc.sync.dma_start(out=h_sb[i][:], in_=h_tiles[i])
+            nc.sync.dma_start(out=x_sb[i][:], in_=x_tiles[i])
+
+        def spread(row, bank):
+            for j in range(BANKS):
+                cols = slice(j * BANK, (j + 1) * BANK)
+                nc.tensor.matmul(out=bank[:, cols], lhsT=ones[:], rhs=row[:, cols], start=True, stop=True)
+
+        b_bank = psum_stage.tile([P, N], BF16, tag="stage")
+        spread(b_row, b_bank)
+        b_all = keep.tile([P, N], BF16)
+        nc.scalar.copy(out=b_all[:], in_=b_bank[:])
+        shift_bank = psum_stage.tile([P, N], BF16, tag="stage")
+        spread(shift_row, shift_bank)
+        shift_all = keep.tile([P, N], BF16)
+        nc.scalar.copy(out=shift_all[:], in_=shift_bank[:])
+        gain_all = psum_gain.tile([P, N], BF16)
+        spread(gain_row, gain_all)
+
+        h_codes = keep.tile([P, TOKEN_TILES, PASSES * P], U32, align_bytes=64)
+        h_scales = keep.tile([P, TOKEN_TILES, PASSES * P], U8, align_bytes=64)
+
+        for i in range(TOKEN_TILES):
+            x_shift = rows.tile([P, N], F32)
+            nc.gpsimd.tensor_tensor(out=x_shift[:], in0=x_sb[i][:], in1=shift_all[:], op=ALU.add)
+
+            h_words = h_sb[i][:].bitcast(F32)
+            flipped = psum_stage.tile([P, PASSES, 2, P], F32, tag="stage")
+            for g in range(PASSES):
+                for u in range(2):
+                    nc.tensor.transpose(
+                        out=flipped[:, g, u, :],
+                        in_=h_words[:, g * WORDS + u : (g + 1) * WORDS : 2],
+                        identity=identity[:],
+                    )
+            grouped = rows.tile([P, PASSES * P * PACK], BF16, align_bytes=64)
+            nc.scalar.copy(
+                out=grouped[:].bitcast(F32).rearrange("p (g r u) -> p g r u", g=PASSES, u=2),
+                in_=flipped[:].rearrange("p g u r -> p g r u"),
+            )
+            nc.vector.quantize_mx(
+                out=h_codes[:, i, :].bitcast(FP8X4), scales=h_scales[:, i, :], in_=grouped[:]
+            )
+
+            o_sb = rows.tile([P, N], F32)
+            row_sum = small.tile([P, BANKS], F32)
+            for j in range(BANKS):
+                acc = psum_acc.tile([P, BANK], F32)
+                for g in range(PASSES):
+                    nc.tensor.matmul_mx(
+                        out=acc[:],
+                        lhsT=h_codes[:, i, g * P : (g + 1) * P].bitcast(FP8X4),
+                        lhsT_scale=h_scales[:, i, g * P : (g + 1) * P],
+                        rhs=w_words[:, g, 2 * j * BANK : 2 * (j + 1) * BANK].bitcast(FP4X4),
+                        rhs_scale=w_scales[:, g, j * BANK : (j + 1) * BANK],
+                        start=(g == 0),
+                        stop=(g == PASSES - 1),
+                    )
+                cols = slice(j * BANK, (j + 1) * BANK)
+                nc.vector.scalar_tensor_tensor(
+                    out=o_sb[:, cols],
+                    in0=acc[:],
+                    scalar=1.0,
+                    in1=b_all[:, cols],
+                    op0=ALU.mult,
+                    op1=ALU.add,
+                    accum_out=row_sum[:, j : j + 1],
+                )
+
+            neg_mean = small.tile([P, 1], F32)
+            nc.vector.tensor_scalar(
+                out=neg_mean[:],
+                in0=row_sum[:, 0:1],
+                scalar1=row_sum[:, 1:2],
+                scalar2=-1.0 / N,
+                op0=ALU.add,
+                op1=ALU.mult,
+            )
+            squares = rows.tile([P, N], BF16)
+            sum_squares = small.tile([P, 1], F32)
+            nc.scalar.activation(
+                out=squares[:], in_=o_sb[:], func=ACT.Square, bias=neg_mean[:], accum_out=sum_squares[:]
+            )
+            centred_gain = rows.tile([P, N], F32)
+            nc.vector.scalar_tensor_tensor(
+                out=centred_gain[:],
+                in0=o_sb[:],
+                scalar=neg_mean[:],
+                in1=gain_all[:],
+                op0=ALU.add,
+                op1=ALU.mult,
+            )
+            std = small.tile([P, 1], F32)
+            nc.scalar.activation(out=std[:], in_=sum_squares[:], func=ACT.Sqrt, scale=1.0 / N, bias=eps[:])
+            rstd = small.tile([P, 1], F32)
+            nc.vector.reciprocal(out=rstd[:], in_=std[:])
+
+            result = rows.tile([P, N], F32)
+            nc.vector.scalar_tensor_tensor(
+                out=result[:],
+                in0=centred_gain[:],
+                scalar=rstd[:],
+                in1=x_shift[:],
+                op0=ALU.mult,
+                op1=ALU.add,
+            )
+            nc.sync.dma_start(out=out_tiles[i], in_=result[:])

@@ -51,73 +51,72 @@ def tile_dcadecoderblock_pb_kernel(
         small = ctx.enter_context(tc.tile_pool(name="small", bufs=TOKEN_TILES))
         psum_gain = ctx.enter_context(tc.psum_pool(name="psum_gain", bufs=1))
         psum_stage = ctx.enter_context(tc.psum_pool(name="psum_stage", bufs=3))
-        psum_acc = ctx.enter_context(tc.psum_pool(name="psum_acc", bufs=4))
+        psum_acc = ctx.enter_context(tc.psum_pool(name="psum_acc", bufs=2 * BANKS))
+        ctx.enter_context(tc.manual_schedule())
 
+        w_words = keep.tile([P, PASSES, 2 * N], U8, align_bytes=64)
         w_scales = keep.tile([P, PASSES, N], U8, align_bytes=64)
-        nc.vector.memset(w_scales[:].rearrange("p g n -> p (g n)").bitcast(I32), 0)
+        h_codes = keep.tile([P, TOKEN_TILES, PASSES * P], U32, align_bytes=64)
+        h_scales = keep.tile([P, TOKEN_TILES, PASSES * P], U8, align_bytes=64)
         b_row = keep.tile([P, N], BF16)
-        shift_row = keep.tile([P, N], BF16)
         gain_row = keep.tile([P, N], BF16)
+        shift_row = keep.tile([P, N], BF16)
+        b_all = keep.tile([P, N], BF16)
+        shift_all = keep.tile([P, N], BF16)
+        gain_all = psum_gain.tile([P, N], BF16)
         ones = keep.tile([P, P], BF16)
-        eps = keep.tile([P, 1], F32)
-        nc.vector.memset(b_row[:], 0.0)
-        nc.vector.memset(shift_row[:], 0.0)
-        nc.vector.memset(gain_row[:], 0.0)
-        nc.vector.memset(ones[:], 1.0)
-        nc.vector.memset(eps[:], EPS)
         identity = keep.tile([P, P], F32)
-        make_identity(nc, identity[:])
+        eps = keep.tile([P, 1], F32)
         table_warm = keep.tile([P, 1], F32)
-        nc.scalar.activation(out=table_warm[:], in_=eps[:], func=ACT.Sqrt)
-
         h_sb = []
         x_sb = []
+        x_shift = []
+        o_sb = []
+        neg_mean = []
+        std = []
+        centred_gain = []
         for i in range(TOKEN_TILES):
             h_sb.append(rows.tile([P, K], BF16, name="h_sb"))
             x_sb.append(rows.tile([P, N], BF16, name="x_sb"))
-        w_words = keep.tile([P, PASSES, 2 * N], U8, align_bytes=64)
+            x_shift.append(rows.tile([P, N], F32, name="x_shift"))
+            o_sb.append(rows.tile([P, N], F32, name="o_sb"))
+            neg_mean.append(small.tile([P, 1], F32, name="neg_mean"))
+            std.append(small.tile([P, 1], F32, name="std"))
+            centred_gain.append(rows.tile([P, N], F32, name="centred_gain"))
+
+        nc.vector.memset(b_row[:].bitcast(I32), 0)
+        nc.vector.memset(gain_row[:].bitcast(I32), 0)
+        nc.vector.memset(w_scales[:].rearrange("p g n -> p (g n)").bitcast(I32), 0)
+        nc.vector.memset(eps[:], EPS)
+        nc.vector.memset(ones[:], 1.0)
+        nc.vector.memset(shift_row[:].bitcast(I32), 0)
+        make_identity(nc, identity[:])
 
         nc.sync.dma_start(out=h_sb[0][:], in_=h_tiles[0])
+        nc.scalar.dma_start(out=b_row[0:1, :], in_=attn_out_b.unsqueeze(0))
+        nc.scalar.dma_start(out=gain_row[0:1, :], in_=attn_norm_g.unsqueeze(0))
+        nc.sync.dma_start(
+            out=w_words[:].bitcast(I32),
+            in_=attn_out_W_words.rearrange("g p b -> p g b").bitcast(I32),
+        )
         for q in range(4):
             nc.sync.dma_start(
                 out=w_scales[32 * q : 32 * q + 4, :, :].bitcast(I32),
                 in_=attn_out_W_scales[:, 4 * q : 4 * q + 4, :].rearrange("g r n -> r g n").bitcast(I32),
             )
-        nc.scalar.dma_start(out=b_row[0:1, :], in_=attn_out_b.unsqueeze(0))
-        nc.scalar.dma_start(out=shift_row[0:1, :], in_=attn_norm_b.unsqueeze(0))
-        nc.sync.dma_start(
-            out=w_words[:].bitcast(I32),
-            in_=attn_out_W_words.rearrange("g p b -> p g b").bitcast(I32),
-        )
-        nc.scalar.dma_start(out=gain_row[0:1, :], in_=attn_norm_g.unsqueeze(0))
-        nc.sync.dma_start(out=x_sb[0][:], in_=x_tiles[0])
+        nc.sync.dma_start(out=shift_row[0:1, :], in_=attn_norm_b.unsqueeze(0))
         for i in range(1, TOKEN_TILES):
             nc.sync.dma_start(out=h_sb[i][:], in_=h_tiles[i])
-            nc.sync.dma_start(out=x_sb[i][:], in_=x_tiles[i])
+            nc.sync.dma_start(out=x_sb[i - 1][:], in_=x_tiles[i - 1])
+        nc.sync.dma_start(out=x_sb[TOKEN_TILES - 1][:], in_=x_tiles[TOKEN_TILES - 1])
+        nc.scalar.activation(out=table_warm[:], in_=eps[:], func=ACT.Sqrt)
 
         def spread(row, bank):
             for j in range(BANKS):
                 cols = slice(j * BANK, (j + 1) * BANK)
                 nc.tensor.matmul(out=bank[:, cols], lhsT=ones[:], rhs=row[:, cols], start=True, stop=True)
 
-        b_bank = psum_stage.tile([P, N], BF16, tag="stage")
-        spread(b_row, b_bank)
-        b_all = keep.tile([P, N], BF16)
-        nc.scalar.copy(out=b_all[:], in_=b_bank[:])
-        shift_bank = psum_stage.tile([P, N], BF16, tag="stage")
-        spread(shift_row, shift_bank)
-        shift_all = keep.tile([P, N], BF16)
-        nc.scalar.copy(out=shift_all[:], in_=shift_bank[:])
-        gain_all = psum_gain.tile([P, N], BF16)
-        spread(gain_row, gain_all)
-
-        h_codes = keep.tile([P, TOKEN_TILES, PASSES * P], U32, align_bytes=64)
-        h_scales = keep.tile([P, TOKEN_TILES, PASSES * P], U8, align_bytes=64)
-
-        for i in range(TOKEN_TILES):
-            x_shift = rows.tile([P, N], F32)
-            nc.gpsimd.tensor_tensor(out=x_shift[:], in0=x_sb[i][:], in1=shift_all[:], op=ALU.add)
-
+        def flip(i):
             h_words = h_sb[i][:].bitcast(F32)
             flipped = psum_stage.tile([P, PASSES, 2, P], F32, tag="stage")
             for g in range(PASSES):
@@ -132,12 +131,15 @@ def tile_dcadecoderblock_pb_kernel(
                 out=grouped[:].bitcast(F32).rearrange("p (g r u) -> p g r u", g=PASSES, u=2),
                 in_=flipped[:].rearrange("p g u r -> p g r u"),
             )
+            return grouped
+
+        def quantise(i, grouped):
             nc.vector.quantize_mx(
                 out=h_codes[:, i, :].bitcast(FP8X4), scales=h_scales[:, i, :], in_=grouped[:]
             )
 
-            o_sb = rows.tile([P, N], F32)
-            row_sum = small.tile([P, BANKS], F32)
+        def project(i):
+            banks = []
             for j in range(BANKS):
                 acc = psum_acc.tile([P, BANK], F32)
                 for g in range(PASSES):
@@ -150,52 +152,90 @@ def tile_dcadecoderblock_pb_kernel(
                         start=(g == 0),
                         stop=(g == PASSES - 1),
                     )
+                banks.append(acc)
+            return banks
+
+        def add_bias(i, banks):
+            row_sum = small.tile([P, BANKS], F32)
+            for j in range(BANKS):
                 cols = slice(j * BANK, (j + 1) * BANK)
                 nc.vector.scalar_tensor_tensor(
-                    out=o_sb[:, cols],
-                    in0=acc[:],
+                    out=o_sb[i][:, cols],
+                    in0=banks[j][:],
                     scalar=1.0,
                     in1=b_all[:, cols],
                     op0=ALU.mult,
                     op1=ALU.add,
                     accum_out=row_sum[:, j : j + 1],
                 )
-
-            neg_mean = small.tile([P, 1], F32)
             nc.vector.tensor_scalar(
-                out=neg_mean[:],
+                out=neg_mean[i][:],
                 in0=row_sum[:, 0:1],
                 scalar1=row_sum[:, 1:2],
                 scalar2=-1.0 / N,
                 op0=ALU.add,
                 op1=ALU.mult,
             )
+
+        def deviation(i):
             squares = rows.tile([P, N], BF16)
             sum_squares = small.tile([P, 1], F32)
             nc.scalar.activation(
-                out=squares[:], in_=o_sb[:], func=ACT.Square, bias=neg_mean[:], accum_out=sum_squares[:]
+                out=squares[:], in_=o_sb[i][:], func=ACT.Square, bias=neg_mean[i][:], accum_out=sum_squares[:]
             )
-            centred_gain = rows.tile([P, N], F32)
+            nc.scalar.activation(out=std[i][:], in_=sum_squares[:], func=ACT.Sqrt, scale=1.0 / N, bias=eps[:])
+
+        def apply_gain(i):
             nc.vector.scalar_tensor_tensor(
-                out=centred_gain[:],
-                in0=o_sb[:],
-                scalar=neg_mean[:],
+                out=centred_gain[i][:],
+                in0=o_sb[i][:],
+                scalar=neg_mean[i][:],
                 in1=gain_all[:],
                 op0=ALU.add,
                 op1=ALU.mult,
             )
-            std = small.tile([P, 1], F32)
-            nc.scalar.activation(out=std[:], in_=sum_squares[:], func=ACT.Sqrt, scale=1.0 / N, bias=eps[:])
-            rstd = small.tile([P, 1], F32)
-            nc.vector.reciprocal(out=rstd[:], in_=std[:])
 
+        def finish(i):
+            rstd = small.tile([P, 1], F32)
+            nc.vector.reciprocal(out=rstd[:], in_=std[i][:])
             result = rows.tile([P, N], F32)
-            nc.vector.scalar_tensor_tensor(
-                out=result[:],
-                in0=centred_gain[:],
-                scalar=rstd[:],
-                in1=x_shift[:],
-                op0=ALU.mult,
-                op1=ALU.add,
-            )
-            nc.sync.dma_start(out=out_tiles[i], in_=result[:])
+            for j in range(BANKS):
+                cols = slice(j * BANK, (j + 1) * BANK)
+                nc.vector.scalar_tensor_tensor(
+                    out=result[:, cols],
+                    in0=centred_gain[i][:, cols],
+                    scalar=rstd[:],
+                    in1=x_shift[i][:, cols],
+                    op0=ALU.mult,
+                    op1=ALU.add,
+                )
+                nc.sync.dma_start(out=out_tiles[i][:, cols], in_=result[:, cols])
+
+        grouped = {}
+        banks = {}
+        grouped[0] = flip(0)
+        b_bank = psum_stage.tile([P, N], BF16, tag="stage")
+        spread(b_row, b_bank)
+        nc.scalar.copy(out=b_all[:], in_=b_bank[:])
+        spread(gain_row, gain_all)
+        quantise(0, grouped[0])
+        banks[0] = project(0)
+        grouped[1] = flip(1)
+        shift_bank = psum_stage.tile([P, N], BF16, tag="stage")
+        spread(shift_row, shift_bank)
+        nc.scalar.copy(out=shift_all[:], in_=shift_bank[:])
+        for i in range(TOKEN_TILES):
+            nc.gpsimd.tensor_tensor(out=x_shift[i][:], in0=x_sb[i][:], in1=shift_all[:], op=ALU.add)
+
+        for i in range(TOKEN_TILES):
+            add_bias(i, banks[i])
+            deviation(i)
+            if i + 1 < TOKEN_TILES:
+                quantise(i + 1, grouped[i + 1])
+                banks[i + 1] = project(i + 1)
+            if i + 2 < TOKEN_TILES:
+                grouped[i + 2] = flip(i + 2)
+            if i >= 1:
+                finish(i - 1)
+            apply_gain(i)
+        finish(TOKEN_TILES - 1)

@@ -49,8 +49,8 @@ def tile_dcadecoderblock_pb_kernel(
         keep = ctx.enter_context(tc.tile_pool(name="keep", bufs=1))
         rows = ctx.enter_context(tc.tile_pool(name="rows", bufs=TOKEN_TILES))
         small = ctx.enter_context(tc.tile_pool(name="small", bufs=TOKEN_TILES))
-        psum_gain = ctx.enter_context(tc.psum_pool(name="psum_gain", bufs=1))
-        psum_stage = ctx.enter_context(tc.psum_pool(name="psum_stage", bufs=3))
+        psum_keep = ctx.enter_context(tc.psum_pool(name="psum_keep", bufs=1))
+        psum_stage = ctx.enter_context(tc.psum_pool(name="psum_stage", bufs=2))
         psum_acc = ctx.enter_context(tc.psum_pool(name="psum_acc", bufs=2 * BANKS))
         ctx.enter_context(tc.manual_schedule())
 
@@ -62,8 +62,8 @@ def tile_dcadecoderblock_pb_kernel(
         gain_row = keep.tile([P, N], BF16)
         shift_row = keep.tile([P, N], BF16)
         b_all = keep.tile([P, N], BF16)
-        shift_all = keep.tile([P, N], BF16)
-        gain_all = psum_gain.tile([P, N], BF16)
+        gain_all = psum_keep.tile([P, N], BF16)
+        shift_all = psum_keep.tile([P, N], BF16)
         ones = keep.tile([P, P], BF16)
         identity = keep.tile([P, P], F32)
         eps = keep.tile([P, 1], F32)
@@ -84,17 +84,18 @@ def tile_dcadecoderblock_pb_kernel(
             std.append(small.tile([P, 1], F32, name="std"))
             centred_gain.append(rows.tile([P, N], F32, name="centred_gain"))
 
+        nc.vector.memset(shift_row[:].bitcast(I32), 0)
         nc.vector.memset(b_row[:].bitcast(I32), 0)
-        nc.vector.memset(gain_row[:].bitcast(I32), 0)
         nc.vector.memset(w_scales[:].rearrange("p g n -> p (g n)").bitcast(I32), 0)
         nc.vector.memset(eps[:], EPS)
         nc.vector.memset(ones[:], 1.0)
-        nc.vector.memset(shift_row[:].bitcast(I32), 0)
+        nc.vector.memset(gain_row[:].bitcast(I32), 0)
         make_identity(nc, identity[:])
 
         nc.sync.dma_start(out=h_sb[0][:], in_=h_tiles[0])
+        nc.scalar.dma_start(out=shift_row[0:1, :], in_=attn_norm_b.unsqueeze(0))
         nc.scalar.dma_start(out=b_row[0:1, :], in_=attn_out_b.unsqueeze(0))
-        nc.scalar.dma_start(out=gain_row[0:1, :], in_=attn_norm_g.unsqueeze(0))
+        nc.scalar.activation(out=table_warm[:], in_=eps[:], func=ACT.Sqrt)
         nc.sync.dma_start(
             out=w_words[:].bitcast(I32),
             in_=attn_out_W_words.rearrange("g p b -> p g b").bitcast(I32),
@@ -104,12 +105,11 @@ def tile_dcadecoderblock_pb_kernel(
                 out=w_scales[32 * q : 32 * q + 4, :, :].bitcast(I32),
                 in_=attn_out_W_scales[:, 4 * q : 4 * q + 4, :].rearrange("g r n -> r g n").bitcast(I32),
             )
-        nc.sync.dma_start(out=shift_row[0:1, :], in_=attn_norm_b.unsqueeze(0))
+        nc.scalar.dma_start(out=gain_row[0:1, :], in_=attn_norm_g.unsqueeze(0))
+        nc.sync.dma_start(out=x_sb[0][:], in_=x_tiles[0])
         for i in range(1, TOKEN_TILES):
             nc.sync.dma_start(out=h_sb[i][:], in_=h_tiles[i])
-            nc.sync.dma_start(out=x_sb[i - 1][:], in_=x_tiles[i - 1])
-        nc.sync.dma_start(out=x_sb[TOKEN_TILES - 1][:], in_=x_tiles[TOKEN_TILES - 1])
-        nc.scalar.activation(out=table_warm[:], in_=eps[:], func=ACT.Sqrt)
+            nc.sync.dma_start(out=x_sb[i][:], in_=x_tiles[i])
 
         def spread(row, bank):
             for j in range(BANKS):
@@ -185,6 +185,9 @@ def tile_dcadecoderblock_pb_kernel(
             )
             nc.scalar.activation(out=std[i][:], in_=sum_squares[:], func=ACT.Sqrt, scale=1.0 / N, bias=eps[:])
 
+        def add_shift(i):
+            nc.vector.tensor_tensor(out=x_shift[i][:], in0=x_sb[i][:], in1=shift_all[:], op=ALU.add)
+
         def apply_gain(i):
             nc.vector.scalar_tensor_tensor(
                 out=centred_gain[i][:],
@@ -217,25 +220,21 @@ def tile_dcadecoderblock_pb_kernel(
         b_bank = psum_stage.tile([P, N], BF16, tag="stage")
         spread(b_row, b_bank)
         nc.scalar.copy(out=b_all[:], in_=b_bank[:])
-        spread(gain_row, gain_all)
+        spread(shift_row, shift_all)
         quantise(0, grouped[0])
+        add_shift(0)
         banks[0] = project(0)
         grouped[1] = flip(1)
-        shift_bank = psum_stage.tile([P, N], BF16, tag="stage")
-        spread(shift_row, shift_bank)
-        nc.scalar.copy(out=shift_all[:], in_=shift_bank[:])
-        for i in range(TOKEN_TILES):
-            nc.gpsimd.tensor_tensor(out=x_shift[i][:], in0=x_sb[i][:], in1=shift_all[:], op=ALU.add)
+        spread(gain_row, gain_all)
 
         for i in range(TOKEN_TILES):
             add_bias(i, banks[i])
             deviation(i)
+            apply_gain(i)
             if i + 1 < TOKEN_TILES:
                 quantise(i + 1, grouped[i + 1])
                 banks[i + 1] = project(i + 1)
+                add_shift(i + 1)
             if i + 2 < TOKEN_TILES:
                 grouped[i + 2] = flip(i + 2)
-            if i >= 1:
-                finish(i - 1)
-            apply_gain(i)
-        finish(TOKEN_TILES - 1)
+            finish(i)

@@ -25,6 +25,7 @@ PASSES = K // K_PASS
 BANKS = N // BANK
 WORDS = K_PASS // 2
 EPS = 1e-5
+SHIFT_COLS = 512
 
 FLOPS = 2 * TOKENS * K * N
 
@@ -49,8 +50,8 @@ def tile_dcadecoderblock_pb_kernel(
         keep = ctx.enter_context(tc.tile_pool(name="keep", bufs=1))
         rows = ctx.enter_context(tc.tile_pool(name="rows", bufs=TOKEN_TILES))
         small = ctx.enter_context(tc.tile_pool(name="small", bufs=TOKEN_TILES))
-        psum_keep = ctx.enter_context(tc.psum_pool(name="psum_keep", bufs=1))
-        psum_stage = ctx.enter_context(tc.psum_pool(name="psum_stage", bufs=2))
+        psum_gain = ctx.enter_context(tc.psum_pool(name="psum_gain", bufs=1))
+        psum_stage = ctx.enter_context(tc.psum_pool(name="psum_stage", bufs=3))
         psum_acc = ctx.enter_context(tc.psum_pool(name="psum_acc", bufs=2 * BANKS))
         ctx.enter_context(tc.manual_schedule())
 
@@ -62,8 +63,8 @@ def tile_dcadecoderblock_pb_kernel(
         gain_row = keep.tile([P, N], BF16)
         shift_row = keep.tile([P, N], BF16)
         b_all = keep.tile([P, N], BF16)
-        gain_all = psum_keep.tile([P, N], BF16)
-        shift_all = psum_keep.tile([P, N], BF16)
+        shift_all = keep.tile([P, N], BF16)
+        gain_all = psum_gain.tile([P, N], BF16)
         ones = keep.tile([P, P], BF16)
         identity = keep.tile([P, P], F32)
         eps = keep.tile([P, 1], F32)
@@ -73,7 +74,7 @@ def tile_dcadecoderblock_pb_kernel(
         x_shift = []
         o_sb = []
         neg_mean = []
-        std = []
+        rstd = []
         centred_gain = []
         for i in range(TOKEN_TILES):
             h_sb.append(rows.tile([P, K], BF16, name="h_sb"))
@@ -81,7 +82,7 @@ def tile_dcadecoderblock_pb_kernel(
             x_shift.append(rows.tile([P, N], F32, name="x_shift"))
             o_sb.append(rows.tile([P, N], F32, name="o_sb"))
             neg_mean.append(small.tile([P, 1], F32, name="neg_mean"))
-            std.append(small.tile([P, 1], F32, name="std"))
+            rstd.append(small.tile([P, 1], F32, name="rstd"))
             centred_gain.append(rows.tile([P, N], F32, name="centred_gain"))
 
         nc.vector.memset(shift_row[:].bitcast(I32), 0)
@@ -95,7 +96,7 @@ def tile_dcadecoderblock_pb_kernel(
         nc.sync.dma_start(out=h_sb[0][:], in_=h_tiles[0])
         nc.scalar.dma_start(out=shift_row[0:1, :], in_=attn_norm_b.unsqueeze(0))
         nc.scalar.dma_start(out=b_row[0:1, :], in_=attn_out_b.unsqueeze(0))
-        nc.scalar.activation(out=table_warm[:], in_=eps[:], func=ACT.Sqrt)
+        nc.scalar.activation(out=table_warm[:], in_=eps[:], func=ACT.Abs_reciprocal_sqrt)
         nc.sync.dma_start(
             out=w_words[:].bitcast(I32),
             in_=attn_out_W_words.rearrange("g p b -> p g b").bitcast(I32),
@@ -106,10 +107,10 @@ def tile_dcadecoderblock_pb_kernel(
                 in_=attn_out_W_scales[:, 4 * q : 4 * q + 4, :].rearrange("g r n -> r g n").bitcast(I32),
             )
         nc.scalar.dma_start(out=gain_row[0:1, :], in_=attn_norm_g.unsqueeze(0))
-        nc.sync.dma_start(out=x_sb[0][:], in_=x_tiles[0])
         for i in range(1, TOKEN_TILES):
             nc.sync.dma_start(out=h_sb[i][:], in_=h_tiles[i])
-            nc.sync.dma_start(out=x_sb[i][:], in_=x_tiles[i])
+            nc.sync.dma_start(out=x_sb[i - 1][:], in_=x_tiles[i - 1])
+        nc.sync.dma_start(out=x_sb[TOKEN_TILES - 1][:], in_=x_tiles[TOKEN_TILES - 1])
 
         def spread(row, bank):
             for j in range(BANKS):
@@ -183,10 +184,9 @@ def tile_dcadecoderblock_pb_kernel(
             nc.scalar.activation(
                 out=squares[:], in_=o_sb[i][:], func=ACT.Square, bias=neg_mean[i][:], accum_out=sum_squares[:]
             )
-            nc.scalar.activation(out=std[i][:], in_=sum_squares[:], func=ACT.Sqrt, scale=1.0 / N, bias=eps[:])
-
-        def add_shift(i):
-            nc.vector.tensor_tensor(out=x_shift[i][:], in0=x_sb[i][:], in1=shift_all[:], op=ALU.add)
+            nc.scalar.activation(
+                out=rstd[i][:], in_=sum_squares[:], func=ACT.Abs_reciprocal_sqrt, scale=1.0 / N, bias=eps[:]
+            )
 
         def apply_gain(i):
             nc.vector.scalar_tensor_tensor(
@@ -199,15 +199,13 @@ def tile_dcadecoderblock_pb_kernel(
             )
 
         def finish(i):
-            rstd = small.tile([P, 1], F32)
-            nc.vector.reciprocal(out=rstd[:], in_=std[i][:])
             result = rows.tile([P, N], F32)
             for j in range(BANKS):
                 cols = slice(j * BANK, (j + 1) * BANK)
                 nc.vector.scalar_tensor_tensor(
                     out=result[:, cols],
                     in0=centred_gain[i][:, cols],
-                    scalar=rstd[:],
+                    scalar=rstd[i][:],
                     in1=x_shift[i][:, cols],
                     op0=ALU.mult,
                     op1=ALU.add,
@@ -220,21 +218,29 @@ def tile_dcadecoderblock_pb_kernel(
         b_bank = psum_stage.tile([P, N], BF16, tag="stage")
         spread(b_row, b_bank)
         nc.scalar.copy(out=b_all[:], in_=b_bank[:])
-        spread(shift_row, shift_all)
+        shift_bank = psum_stage.tile([P, N], BF16, tag="stage")
+        spread(shift_row, shift_bank)
+        nc.scalar.copy(out=shift_all[:], in_=shift_bank[:])
         quantise(0, grouped[0])
-        add_shift(0)
         banks[0] = project(0)
         grouped[1] = flip(1)
         spread(gain_row, gain_all)
 
         for i in range(TOKEN_TILES):
+            for c in range(0, N, SHIFT_COLS):
+                cols = slice(c, c + SHIFT_COLS)
+                nc.gpsimd.tensor_tensor(
+                    out=x_shift[i][:, cols], in0=x_sb[i][:, cols], in1=shift_all[:, cols], op=ALU.add
+                )
+
+        for i in range(TOKEN_TILES):
             add_bias(i, banks[i])
             deviation(i)
-            apply_gain(i)
             if i + 1 < TOKEN_TILES:
                 quantise(i + 1, grouped[i + 1])
                 banks[i + 1] = project(i + 1)
-                add_shift(i + 1)
             if i + 2 < TOKEN_TILES:
                 grouped[i + 2] = flip(i + 2)
+            apply_gain(i)
+        for i in range(TOKEN_TILES):
             finish(i)

@@ -215,12 +215,12 @@ def tile_dcadecoderblock_pb_kernel(
         grouped = {}
         banks = {}
         grouped[0] = flip(0)
-        b_bank = psum_stage.tile([P, N], BF16, tag="stage")
-        spread(b_row, b_bank)
-        nc.scalar.copy(out=b_all[:], in_=b_bank[:])
         shift_bank = psum_stage.tile([P, N], BF16, tag="stage")
         spread(shift_row, shift_bank)
         nc.scalar.copy(out=shift_all[:], in_=shift_bank[:])
+        b_bank = psum_stage.tile([P, N], BF16, tag="stage")
+        spread(b_row, b_bank)
+        nc.scalar.copy(out=b_all[:], in_=b_bank[:])
         quantise(0, grouped[0])
         banks[0] = project(0)
         grouped[1] = flip(1)

@@ -222,8 +222,8 @@ def tile_dcadecoderblock_pb_kernel(
         spread(b_row, b_bank)
         nc.scalar.copy(out=b_all[:], in_=b_bank[:])
         quantise(0, grouped[0])
-        banks[0] = project(0)
         grouped[1] = flip(1)
+        banks[0] = project(0)
         spread(gain_row, gain_all)
 
         for i in range(TOKEN_TILES):
@@ -234,13 +234,13 @@ def tile_dcadecoderblock_pb_kernel(
                 )
 
         for i in range(TOKEN_TILES):
-            add_bias(i, banks[i])
-            deviation(i)
             if i + 1 < TOKEN_TILES:
                 quantise(i + 1, grouped[i + 1])
                 banks[i + 1] = project(i + 1)
             if i + 2 < TOKEN_TILES:
                 grouped[i + 2] = flip(i + 2)
+            add_bias(i, banks[i])
+            deviation(i)
             apply_gain(i)
         for i in range(TOKEN_TILES):
             finish(i)

@@ -25,7 +25,9 @@ PASSES = K // K_PASS
 BANKS = N // BANK
 WORDS = K_PASS // 2
 EPS = 1e-5
-SHIFT_COLS = 512
+FEATURE_BLOCKS = N // P
+BLOCKS_PER_BANK = BANK // P
+BLOCKS_PER_TILE = 3
 
 FLOPS = 2 * TOKENS * K * N
 
@@ -50,7 +52,7 @@ def tile_dcadecoderblock_pb_kernel(
         keep = ctx.enter_context(tc.tile_pool(name="keep", bufs=1))
         rows = ctx.enter_context(tc.tile_pool(name="rows", bufs=TOKEN_TILES))
         small = ctx.enter_context(tc.tile_pool(name="small", bufs=TOKEN_TILES))
-        psum_gain = ctx.enter_context(tc.psum_pool(name="psum_gain", bufs=1))
+        psum_keep = ctx.enter_context(tc.psum_pool(name="psum_keep", bufs=1))
         psum_stage = ctx.enter_context(tc.psum_pool(name="psum_stage", bufs=3))
         psum_acc = ctx.enter_context(tc.psum_pool(name="psum_acc", bufs=2 * BANKS))
         ctx.enter_context(tc.manual_schedule())
@@ -61,17 +63,18 @@ def tile_dcadecoderblock_pb_kernel(
         h_scales = keep.tile([P, TOKEN_TILES, PASSES * P], U8, align_bytes=64)
         b_row = keep.tile([P, N], BF16)
         gain_row = keep.tile([P, N], BF16)
-        shift_row = keep.tile([P, N], BF16)
         b_all = keep.tile([P, N], BF16)
-        shift_all = keep.tile([P, N], BF16)
-        gain_all = psum_gain.tile([P, N], BF16)
+        gain_all = psum_keep.tile([P, N], BF16)
+        shift_rows = keep.tile([P, P], BF16)
+        shift_cols = keep.tile([P, FEATURE_BLOCKS], F32)
+        x_shift_t = keep.tile([P, FEATURE_BLOCKS, TOKENS], F32)
         ones = keep.tile([P, P], BF16)
         identity = keep.tile([P, P], F32)
+        identity_bf = keep.tile([P, P], BF16)
         eps = keep.tile([P, 1], F32)
         table_warm = keep.tile([P, 1], F32)
         h_sb = []
         x_sb = []
-        x_shift = []
         o_sb = []
         neg_mean = []
         rstd = []
@@ -79,23 +82,25 @@ def tile_dcadecoderblock_pb_kernel(
         for i in range(TOKEN_TILES):
             h_sb.append(rows.tile([P, K], BF16, name="h_sb"))
             x_sb.append(rows.tile([P, N], BF16, name="x_sb"))
-            x_shift.append(rows.tile([P, N], F32, name="x_shift"))
             o_sb.append(rows.tile([P, N], F32, name="o_sb"))
             neg_mean.append(small.tile([P, 1], F32, name="neg_mean"))
             rstd.append(small.tile([P, 1], F32, name="rstd"))
             centred_gain.append(rows.tile([P, N], F32, name="centred_gain"))
 
-        nc.vector.memset(shift_row[:].bitcast(I32), 0)
         nc.vector.memset(b_row[:].bitcast(I32), 0)
+        nc.vector.memset(shift_rows[:].bitcast(I32), 0)
         nc.vector.memset(w_scales[:].rearrange("p g n -> p (g n)").bitcast(I32), 0)
         nc.vector.memset(eps[:], EPS)
         nc.vector.memset(ones[:], 1.0)
         nc.vector.memset(gain_row[:].bitcast(I32), 0)
         make_identity(nc, identity[:])
+        make_identity(nc, identity_bf[:])
 
         nc.sync.dma_start(out=h_sb[0][:], in_=h_tiles[0])
-        nc.scalar.dma_start(out=shift_row[0:1, :], in_=attn_norm_b.unsqueeze(0))
         nc.scalar.dma_start(out=b_row[0:1, :], in_=attn_out_b.unsqueeze(0))
+        nc.scalar.dma_start(
+            out=shift_rows[0:FEATURE_BLOCKS, :], in_=attn_norm_b.rearrange("(f p) -> f p", p=P)
+        )
         nc.scalar.activation(out=table_warm[:], in_=eps[:], func=ACT.Abs_reciprocal_sqrt)
         nc.sync.dma_start(
             out=w_words[:].bitcast(I32),
@@ -107,10 +112,11 @@ def tile_dcadecoderblock_pb_kernel(
                 in_=attn_out_W_scales[:, 4 * q : 4 * q + 4, :].rearrange("g r n -> r g n").bitcast(I32),
             )
         nc.scalar.dma_start(out=gain_row[0:1, :], in_=attn_norm_g.unsqueeze(0))
-        for i in range(1, TOKEN_TILES):
+        nc.sync.dma_start(out=h_sb[1][:], in_=h_tiles[1])
+        for i in range(TOKEN_TILES):
+            nc.sync.dma_start(out=x_sb[i][:], in_=x_tiles[i])
+        for i in range(2, TOKEN_TILES):
             nc.sync.dma_start(out=h_sb[i][:], in_=h_tiles[i])
-            nc.sync.dma_start(out=x_sb[i - 1][:], in_=x_tiles[i - 1])
-        nc.sync.dma_start(out=x_sb[TOKEN_TILES - 1][:], in_=x_tiles[TOKEN_TILES - 1])
 
         def spread(row, bank):
             for j in range(BANKS):
@@ -198,15 +204,34 @@ def tile_dcadecoderblock_pb_kernel(
                 op1=ALU.mult,
             )
 
+        def add_shift(f):
+            x_flipped = psum_stage.tile([P, TOKENS], BF16, tag="stage")
+            for i in range(TOKEN_TILES):
+                nc.tensor.transpose(
+                    out=x_flipped[:, i * P : (i + 1) * P],
+                    in_=x_sb[i][:, f * P : (f + 1) * P],
+                    identity=identity_bf[:],
+                )
+            nc.scalar.activation(
+                out=x_shift_t[:, f, :], in_=x_flipped[:], func=ACT.Identity, bias=shift_cols[:, f : f + 1]
+            )
+
         def finish(i):
             result = rows.tile([P, N], F32)
             for j in range(BANKS):
+                x_shift = psum_acc.tile([P, BANK], F32, tag="acc")
+                for m in range(BLOCKS_PER_BANK):
+                    nc.tensor.transpose(
+                        out=x_shift[:, m * P : (m + 1) * P],
+                        in_=x_shift_t[:, j * BLOCKS_PER_BANK + m, i * P : (i + 1) * P],
+                        identity=identity[:],
+                    )
                 cols = slice(j * BANK, (j + 1) * BANK)
                 nc.vector.scalar_tensor_tensor(
                     out=result[:, cols],
                     in0=centred_gain[i][:, cols],
                     scalar=rstd[i][:],
-                    in1=x_shift[i][:, cols],
+                    in1=x_shift[:],
                     op0=ALU.mult,
                     op1=ALU.add,
                 )
@@ -215,23 +240,18 @@ def tile_dcadecoderblock_pb_kernel(
         grouped = {}
         banks = {}
         grouped[0] = flip(0)
-        shift_bank = psum_stage.tile([P, N], BF16, tag="stage")
-        spread(shift_row, shift_bank)
-        nc.scalar.copy(out=shift_all[:], in_=shift_bank[:])
         b_bank = psum_stage.tile([P, N], BF16, tag="stage")
         spread(b_row, b_bank)
         nc.scalar.copy(out=b_all[:], in_=b_bank[:])
+        shift_flipped = psum_stage.tile([P, P], BF16, tag="stage")
+        nc.tensor.transpose(out=shift_flipped[:], in_=shift_rows[:], identity=identity_bf[:])
+        nc.scalar.copy(out=shift_cols[:], in_=shift_flipped[:, 0:FEATURE_BLOCKS])
         quantise(0, grouped[0])
-        grouped[1] = flip(1)
         banks[0] = project(0)
+        grouped[1] = flip(1)
         spread(gain_row, gain_all)
-
-        for i in range(TOKEN_TILES):
-            for c in range(0, N, SHIFT_COLS):
-                cols = slice(c, c + SHIFT_COLS)
-                nc.gpsimd.tensor_tensor(
-                    out=x_shift[i][:, cols], in0=x_sb[i][:, cols], in1=shift_all[:, cols], op=ALU.add
-                )
+        add_bias(0, banks[0])
+        deviation(0)
 
         for i in range(TOKEN_TILES):
             if i + 1 < TOKEN_TILES:
@@ -239,8 +259,12 @@ def tile_dcadecoderblock_pb_kernel(
                 banks[i + 1] = project(i + 1)
             if i + 2 < TOKEN_TILES:
                 grouped[i + 2] = flip(i + 2)
-            add_bias(i, banks[i])
-            deviation(i)
             apply_gain(i)
+            for f in range(i * BLOCKS_PER_TILE, min((i + 1) * BLOCKS_PER_TILE, FEATURE_BLOCKS)):
+                add_shift(f)
+            if i + 1 < TOKEN_TILES:
+                add_bias(i + 1, banks[i + 1])
+        for i in range(1, TOKEN_TILES):
+            deviation(i)
         for i in range(TOKEN_TILES):
             finish(i)

@@ -55,7 +55,6 @@ def tile_dcadecoderblock_pb_kernel(
         psum_keep = ctx.enter_context(tc.psum_pool(name="psum_keep", bufs=1))
         psum_stage = ctx.enter_context(tc.psum_pool(name="psum_stage", bufs=3))
         psum_acc = ctx.enter_context(tc.psum_pool(name="psum_acc", bufs=2 * BANKS))
-        ctx.enter_context(tc.manual_schedule())
 
         w_words = keep.tile([P, PASSES, 2 * N], U8, align_bytes=64)
         w_scales = keep.tile([P, PASSES, N], U8, align_bytes=64)

@@ -27,7 +27,10 @@ WORDS = K_PASS // 2
 EPS = 1e-5
 FEATURE_BLOCKS = N // P
 BLOCKS_PER_BANK = BANK // P
-BLOCKS_PER_TILE = 3
+PSUM_BANKS = 8
+
+VECTOR_HALVES = ((0, 0), (0, 1))
+VECTOR_NORMALISES = (3,)
 
 FLOPS = 2 * TOKENS * K * N
 
@@ -45,86 +48,81 @@ def tile_dcadecoderblock_pb_kernel(
 ):
     nc = tc.nc
     h_tiles = h_attn.flatten_outer_dims().rearrange("(i p) k -> i p k", p=P)
-    x_tiles = x.flatten_outer_dims().rearrange("(i p) n -> i p n", p=P)
     out_tiles = out.flatten_outer_dims().rearrange("(i p) n -> i p n", p=P)
 
     with ExitStack() as ctx:
         keep = ctx.enter_context(tc.tile_pool(name="keep", bufs=1))
         rows = ctx.enter_context(tc.tile_pool(name="rows", bufs=TOKEN_TILES))
         small = ctx.enter_context(tc.tile_pool(name="small", bufs=TOKEN_TILES))
-        psum_keep = ctx.enter_context(tc.psum_pool(name="psum_keep", bufs=1))
-        psum_stage = ctx.enter_context(tc.psum_pool(name="psum_stage", bufs=3))
-        psum_acc = ctx.enter_context(tc.psum_pool(name="psum_acc", bufs=2 * BANKS))
+        psum = ctx.enter_context(tc.psum_pool(name="psum", bufs=PSUM_BANKS))
 
         w_words = keep.tile([P, PASSES, 2 * N], U8, align_bytes=64)
         w_scales = keep.tile([P, PASSES, N], U8, align_bytes=64)
         h_codes = keep.tile([P, TOKEN_TILES, PASSES * P], U32, align_bytes=64)
         h_scales = keep.tile([P, TOKEN_TILES, PASSES * P], U8, align_bytes=64)
+        x_sb = keep.tile([P, TOKEN_TILES, N], BF16)
         b_row = keep.tile([P, N], BF16)
-        gain_row = keep.tile([P, N], BF16)
         b_all = keep.tile([P, N], BF16)
-        gain_all = psum_keep.tile([P, N], BF16)
-        shift_rows = keep.tile([P, P], BF16)
-        shift_cols = keep.tile([P, FEATURE_BLOCKS], F32)
-        x_shift_t = keep.tile([P, FEATURE_BLOCKS, TOKENS], F32)
+        gain_shift_rows = keep.tile([P, P], BF16)
+        gain_shift = keep.tile([P, 2 * FEATURE_BLOCKS], F32)
         ones = keep.tile([P, P], BF16)
         identity = keep.tile([P, P], F32)
         identity_bf = keep.tile([P, P], BF16)
         eps = keep.tile([P, 1], F32)
         table_warm = keep.tile([P, 1], F32)
         h_sb = []
-        x_sb = []
         o_sb = []
+        y_sb = []
+        z_t = []
+        result = []
+        row_sum = []
         neg_mean = []
         rstd = []
-        centred_gain = []
         for i in range(TOKEN_TILES):
             h_sb.append(rows.tile([P, K], BF16, name="h_sb"))
-            x_sb.append(rows.tile([P, N], BF16, name="x_sb"))
             o_sb.append(rows.tile([P, N], F32, name="o_sb"))
+            y_sb.append(rows.tile([P, N], F32, name="y_sb"))
+            z_t.append(rows.tile([P, FEATURE_BLOCKS, P], F32, name="z_t"))
+            result.append(rows.tile([P, N], F32, name="result"))
+            row_sum.append(small.tile([P, BANKS], F32, name="row_sum"))
             neg_mean.append(small.tile([P, 1], F32, name="neg_mean"))
             rstd.append(small.tile([P, 1], F32, name="rstd"))
-            centred_gain.append(rows.tile([P, N], F32, name="centred_gain"))
 
-        nc.vector.memset(b_row[:].bitcast(I32), 0)
-        nc.vector.memset(shift_rows[:].bitcast(I32), 0)
         nc.vector.memset(w_scales[:].rearrange("p g n -> p (g n)").bitcast(I32), 0)
+        nc.vector.memset(b_row[:].bitcast(I32), 0)
+        nc.vector.memset(gain_shift_rows[:].bitcast(I32), 0)
         nc.vector.memset(eps[:], EPS)
         nc.vector.memset(ones[:], 1.0)
-        nc.vector.memset(gain_row[:].bitcast(I32), 0)
         make_identity(nc, identity[:])
         make_identity(nc, identity_bf[:])
 
         nc.sync.dma_start(out=h_sb[0][:], in_=h_tiles[0])
         nc.scalar.dma_start(out=b_row[0:1, :], in_=attn_out_b.unsqueeze(0))
         nc.scalar.dma_start(
-            out=shift_rows[0:FEATURE_BLOCKS, :], in_=attn_norm_b.rearrange("(f p) -> f p", p=P)
+            out=gain_shift_rows[0:FEATURE_BLOCKS, :], in_=attn_norm_g.rearrange("(f p) -> f p", p=P)
+        )
+        nc.scalar.dma_start(
+            out=gain_shift_rows[FEATURE_BLOCKS : 2 * FEATURE_BLOCKS, :],
+            in_=attn_norm_b.rearrange("(f p) -> f p", p=P),
         )
         nc.scalar.activation(out=table_warm[:], in_=eps[:], func=ACT.Abs_reciprocal_sqrt)
-        nc.sync.dma_start(
-            out=w_words[:].bitcast(I32),
-            in_=attn_out_W_words.rearrange("g p b -> p g b").bitcast(I32),
-        )
         for q in range(4):
             nc.sync.dma_start(
                 out=w_scales[32 * q : 32 * q + 4, :, :].bitcast(I32),
                 in_=attn_out_W_scales[:, 4 * q : 4 * q + 4, :].rearrange("g r n -> r g n").bitcast(I32),
             )
-        nc.scalar.dma_start(out=gain_row[0:1, :], in_=attn_norm_g.unsqueeze(0))
         nc.sync.dma_start(out=h_sb[1][:], in_=h_tiles[1])
-        for i in range(TOKEN_TILES):
-            nc.sync.dma_start(out=x_sb[i][:], in_=x_tiles[i])
+        nc.sync.dma_start(
+            out=w_words[:].bitcast(I32),
+            in_=attn_out_W_words.rearrange("g p b -> p g b").bitcast(I32),
+        )
         for i in range(2, TOKEN_TILES):
             nc.sync.dma_start(out=h_sb[i][:], in_=h_tiles[i])
-
-        def spread(row, bank):
-            for j in range(BANKS):
-                cols = slice(j * BANK, (j + 1) * BANK)
-                nc.tensor.matmul(out=bank[:, cols], lhsT=ones[:], rhs=row[:, cols], start=True, stop=True)
+        nc.sync.dma_start(out=x_sb[:], in_=x.flatten_outer_dims().rearrange("(i p) n -> p i n", p=P))
 
         def flip(i):
             h_words = h_sb[i][:].bitcast(F32)
-            flipped = psum_stage.tile([P, PASSES, 2, P], F32, tag="stage")
+            flipped = psum.tile([P, PASSES, 2, P], F32, tag="bank")
             for g in range(PASSES):
                 for u in range(2):
                     nc.tensor.transpose(
@@ -147,7 +145,7 @@ def tile_dcadecoderblock_pb_kernel(
         def project(i):
             banks = []
             for j in range(BANKS):
-                acc = psum_acc.tile([P, BANK], F32)
+                acc = psum.tile([P, BANK], F32, tag="bank")
                 for g in range(PASSES):
                     nc.tensor.matmul_mx(
                         out=acc[:],
@@ -162,7 +160,6 @@ def tile_dcadecoderblock_pb_kernel(
             return banks
 
         def add_bias(i, banks):
-            row_sum = small.tile([P, BANKS], F32)
             for j in range(BANKS):
                 cols = slice(j * BANK, (j + 1) * BANK)
                 nc.vector.scalar_tensor_tensor(
@@ -172,12 +169,12 @@ def tile_dcadecoderblock_pb_kernel(
                     in1=b_all[:, cols],
                     op0=ALU.mult,
                     op1=ALU.add,
-                    accum_out=row_sum[:, j : j + 1],
+                    accum_out=row_sum[i][:, j : j + 1],
                 )
-            nc.vector.tensor_scalar(
+            nc.gpsimd.tensor_scalar(
                 out=neg_mean[i][:],
-                in0=row_sum[:, 0:1],
-                scalar1=row_sum[:, 1:2],
+                in0=row_sum[i][:, 0:1],
+                scalar1=row_sum[i][:, 1:2],
                 scalar2=-1.0 / N,
                 op0=ALU.add,
                 op1=ALU.mult,
@@ -193,77 +190,112 @@ def tile_dcadecoderblock_pb_kernel(
                 out=rstd[i][:], in_=sum_squares[:], func=ACT.Abs_reciprocal_sqrt, scale=1.0 / N, bias=eps[:]
             )
 
-        def apply_gain(i):
-            nc.vector.scalar_tensor_tensor(
-                out=centred_gain[i][:],
-                in0=o_sb[i][:],
-                scalar=neg_mean[i][:],
-                in1=gain_all[:],
-                op0=ALU.add,
-                op1=ALU.mult,
-            )
-
-        def add_shift(f):
-            x_flipped = psum_stage.tile([P, TOKENS], BF16, tag="stage")
-            for i in range(TOKEN_TILES):
-                nc.tensor.transpose(
-                    out=x_flipped[:, i * P : (i + 1) * P],
-                    in_=x_sb[i][:, f * P : (f + 1) * P],
-                    identity=identity_bf[:],
-                )
-            nc.scalar.activation(
-                out=x_shift_t[:, f, :], in_=x_flipped[:], func=ACT.Identity, bias=shift_cols[:, f : f + 1]
-            )
-
-        def finish(i):
-            result = rows.tile([P, N], F32)
-            for j in range(BANKS):
-                x_shift = psum_acc.tile([P, BANK], F32, tag="acc")
-                for m in range(BLOCKS_PER_BANK):
-                    nc.tensor.transpose(
-                        out=x_shift[:, m * P : (m + 1) * P],
-                        in_=x_shift_t[:, j * BLOCKS_PER_BANK + m, i * P : (i + 1) * P],
-                        identity=identity[:],
+        def normalise(i):
+            if i in VECTOR_NORMALISES:
+                for j in range(BANKS):
+                    cols = slice(j * BANK, (j + 1) * BANK)
+                    nc.vector.tensor_scalar(
+                        out=y_sb[i][:, cols],
+                        in0=o_sb[i][:, cols],
+                        scalar1=neg_mean[i][:],
+                        scalar2=rstd[i][:],
+                        op0=ALU.add,
+                        op1=ALU.mult,
                     )
+                return
+            neg_mean_over_std = small.tile([P, 1], F32)
+            nc.gpsimd.tensor_scalar(
+                out=neg_mean_over_std[:],
+                in0=neg_mean[i][:],
+                scalar1=rstd[i][:],
+                scalar2=0.0,
+                op0=ALU.mult,
+                op1=ALU.add,
+            )
+            for j in range(BANKS):
                 cols = slice(j * BANK, (j + 1) * BANK)
-                nc.vector.scalar_tensor_tensor(
-                    out=result[:, cols],
-                    in0=centred_gain[i][:, cols],
-                    scalar=rstd[i][:],
-                    in1=x_shift[:],
+                nc.gpsimd.tensor_scalar(
+                    out=y_sb[i][:, cols],
+                    in0=o_sb[i][:, cols],
+                    scalar1=rstd[i][:],
+                    scalar2=neg_mean_over_std[:],
                     op0=ALU.mult,
                     op1=ALU.add,
                 )
-                nc.sync.dma_start(out=out_tiles[i][:, cols], in_=result[:, cols])
+
+        def scale_shift(i, j):
+            y_t = psum.tile([P, BLOCKS_PER_BANK, P], F32, tag="bank")
+            for m in range(BLOCKS_PER_BANK):
+                f = j * BLOCKS_PER_BANK + m
+                nc.tensor.transpose(out=y_t[:, m, :], in_=y_sb[i][:, f * P : (f + 1) * P], identity=identity[:])
+            for m in range(BLOCKS_PER_BANK):
+                f = j * BLOCKS_PER_BANK + m
+                gain = gain_shift[:, f : f + 1]
+                shift = gain_shift[:, FEATURE_BLOCKS + f : FEATURE_BLOCKS + f + 1]
+                if (i, j) in VECTOR_HALVES:
+                    nc.vector.tensor_scalar(
+                        out=z_t[i][:, f, :], in0=y_t[:, m, :], scalar1=gain, scalar2=shift, op0=ALU.mult, op1=ALU.add
+                    )
+                else:
+                    nc.scalar.activation(out=z_t[i][:, f, :], in_=y_t[:, m, :], func=ACT.Identity, scale=gain, bias=shift)
+
+        def finish(i, j):
+            z = psum.tile([P, BANK], F32, tag="bank")
+            for m in range(BLOCKS_PER_BANK):
+                nc.tensor.transpose(
+                    out=z[:, m * P : (m + 1) * P], in_=z_t[i][:, j * BLOCKS_PER_BANK + m, :], identity=identity[:]
+                )
+            cols = slice(j * BANK, (j + 1) * BANK)
+            nc.vector.tensor_tensor(out=result[i][:, cols], in0=z[:], in1=x_sb[:, i, cols], op=ALU.add)
+            nc.sync.dma_start(out=out_tiles[i][:, cols], in_=result[i][:, cols])
 
         grouped = {}
         banks = {}
         grouped[0] = flip(0)
-        b_bank = psum_stage.tile([P, N], BF16, tag="stage")
-        spread(b_row, b_bank)
-        nc.scalar.copy(out=b_all[:], in_=b_bank[:])
-        shift_flipped = psum_stage.tile([P, P], BF16, tag="stage")
-        nc.tensor.transpose(out=shift_flipped[:], in_=shift_rows[:], identity=identity_bf[:])
-        nc.scalar.copy(out=shift_cols[:], in_=shift_flipped[:, 0:FEATURE_BLOCKS])
+        b_bank = psum.tile([P, N], BF16, tag="bank")
+        for j in range(BANKS):
+            cols = slice(j * BANK, (j + 1) * BANK)
+            nc.tensor.matmul(out=b_bank[:, cols], lhsT=ones[:], rhs=b_row[:, cols], start=True, stop=True)
+        gain_shift_flipped = psum.tile([P, P], BF16, tag="bank")
+        nc.tensor.transpose(out=gain_shift_flipped[:], in_=gain_shift_rows[:], identity=identity_bf[:])
+        nc.scalar.copy(out=gain_shift[:], in_=gain_shift_flipped[:, 0 : 2 * FEATURE_BLOCKS])
         quantise(0, grouped[0])
-        banks[0] = project(0)
+        nc.vector.tensor_copy(out=b_all[:], in_=b_bank[:])
         grouped[1] = flip(1)
-        spread(gain_row, gain_all)
+        banks[0] = project(0)
+        quantise(1, grouped[1])
+        grouped[2] = flip(2)
+        grouped[3] = flip(3)
         add_bias(0, banks[0])
+        banks[1] = project(1)
+        quantise(2, grouped[2])
+        quantise(3, grouped[3])
         deviation(0)
-
-        for i in range(TOKEN_TILES):
-            if i + 1 < TOKEN_TILES:
-                quantise(i + 1, grouped[i + 1])
-                banks[i + 1] = project(i + 1)
-            if i + 2 < TOKEN_TILES:
-                grouped[i + 2] = flip(i + 2)
-            apply_gain(i)
-            for f in range(i * BLOCKS_PER_TILE, min((i + 1) * BLOCKS_PER_TILE, FEATURE_BLOCKS)):
-                add_shift(f)
-            if i + 1 < TOKEN_TILES:
-                add_bias(i + 1, banks[i + 1])
-        for i in range(1, TOKEN_TILES):
-            deviation(i)
-        for i in range(TOKEN_TILES):
-            finish(i)
+        add_bias(1, banks[1])
+        banks[2] = project(2)
+        banks[3] = project(3)
+        deviation(1)
+        add_bias(2, banks[2])
+        normalise(0)
+        deviation(2)
+        add_bias(3, banks[3])
+        deviation(3)
+        scale_shift(0, 0)
+        scale_shift(0, 1)
+        normalise(1)
+        finish(0, 0)
+        finish(0, 1)
+        normalise(3)
+        scale_shift(1, 0)
+        scale_shift(1, 1)
+        normalise(2)
+        scale_shift(3, 0)
+        scale_shift(3, 1)
+        finish(1, 0)
+        finish(1, 1)
+        finish(3, 0)
+        finish(3, 1)
+        scale_shift(2, 0)
+        scale_shift(2, 1)
+        finish(2, 0)
+        finish(2, 1)

@@ -29,8 +29,7 @@ FEATURE_BLOCKS = N // P
 BLOCKS_PER_BANK = BANK // P
 PSUM_BANKS = 8
 
-VECTOR_HALVES = ((0, 0), (0, 1))
-VECTOR_NORMALISES = (3,)
+CLOCK_WARM_MATMULS = 2
 
 FLOPS = 2 * TOKENS * K * N
 
@@ -55,6 +54,7 @@ def tile_dcadecoderblock_pb_kernel(
         rows = ctx.enter_context(tc.tile_pool(name="rows", bufs=TOKEN_TILES))
         small = ctx.enter_context(tc.tile_pool(name="small", bufs=TOKEN_TILES))
         psum = ctx.enter_context(tc.psum_pool(name="psum", bufs=PSUM_BANKS))
+        ctx.enter_context(tc.manual_schedule())
 
         w_words = keep.tile([P, PASSES, 2 * N], U8, align_bytes=64)
         w_scales = keep.tile([P, PASSES, N], U8, align_bytes=64)
@@ -66,33 +66,46 @@ def tile_dcadecoderblock_pb_kernel(
         gain_shift_rows = keep.tile([P, P], BF16)
         gain_shift = keep.tile([P, 2 * FEATURE_BLOCKS], F32)
         ones = keep.tile([P, P], BF16)
+        clock_warm = keep.tile([P, BANK], BF16)
         identity = keep.tile([P, P], F32)
         identity_bf = keep.tile([P, P], BF16)
         eps = keep.tile([P, 1], F32)
         table_warm = keep.tile([P, 1], F32)
         h_sb = []
+        grouped = []
         o_sb = []
         y_sb = []
         z_t = []
         result = []
+        squares = []
         row_sum = []
+        mean_junk = []
         neg_mean = []
+        sum_squares = []
         rstd = []
+        neg_mean_over_std = []
         for i in range(TOKEN_TILES):
             h_sb.append(rows.tile([P, K], BF16, name="h_sb"))
+            grouped.append(rows.tile([P, PASSES * P * PACK], BF16, name="grouped", align_bytes=64))
             o_sb.append(rows.tile([P, N], F32, name="o_sb"))
             y_sb.append(rows.tile([P, N], F32, name="y_sb"))
             z_t.append(rows.tile([P, FEATURE_BLOCKS, P], F32, name="z_t"))
             result.append(rows.tile([P, N], F32, name="result"))
+            squares.append(rows.tile([P, N], BF16, name="squares"))
             row_sum.append(small.tile([P, BANKS], F32, name="row_sum"))
+            mean_junk.append(small.tile([P, BANKS], F32, name="mean_junk"))
             neg_mean.append(small.tile([P, 1], F32, name="neg_mean"))
+            sum_squares.append(small.tile([P, 1], F32, name="sum_squares"))
             rstd.append(small.tile([P, 1], F32, name="rstd"))
+            neg_mean_over_std.append(small.tile([P, 1], F32, name="neg_mean_over_std"))
+        bank_of = {}
 
-        nc.vector.memset(w_scales[:].rearrange("p g n -> p (g n)").bitcast(I32), 0)
+        nc.gpsimd.memset(w_scales[:].rearrange("p g n -> p (g n)").bitcast(F32), 0.0)
+        nc.vector.memset(ones[:], 1.0)
+        nc.vector.memset(clock_warm[:].bitcast(I32), 0)
         nc.vector.memset(b_row[:].bitcast(I32), 0)
         nc.vector.memset(gain_shift_rows[:].bitcast(I32), 0)
         nc.vector.memset(eps[:], EPS)
-        nc.vector.memset(ones[:], 1.0)
         make_identity(nc, identity[:])
         make_identity(nc, identity_bf[:])
 
@@ -111,16 +124,42 @@ def tile_dcadecoderblock_pb_kernel(
                 out=w_scales[32 * q : 32 * q + 4, :, :].bitcast(I32),
                 in_=attn_out_W_scales[:, 4 * q : 4 * q + 4, :].rearrange("g r n -> r g n").bitcast(I32),
             )
-        nc.sync.dma_start(out=h_sb[1][:], in_=h_tiles[1])
         nc.sync.dma_start(
             out=w_words[:].bitcast(I32),
             in_=attn_out_W_words.rearrange("g p b -> p g b").bitcast(I32),
         )
-        for i in range(2, TOKEN_TILES):
-            nc.sync.dma_start(out=h_sb[i][:], in_=h_tiles[i])
+        nc.sync.dma_start(out=h_sb[1][:], in_=h_tiles[1])
+        nc.sync.dma_start(out=h_sb[2][:], in_=h_tiles[2])
+        nc.sync.dma_start(out=h_sb[3][:], in_=h_tiles[3])
         nc.sync.dma_start(out=x_sb[:], in_=x.flatten_outer_dims().rearrange("(i p) n -> p i n", p=P))
 
-        def flip(i):
+        def clock():
+            clock_bank = psum.tile([P, BANK], F32, tag="bank")
+            for r in range(CLOCK_WARM_MATMULS):
+                nc.tensor.matmul(out=clock_bank[:], lhsT=ones[:], rhs=clock_warm[:], start=True, stop=True)
+
+        def spread():
+            b_bank = psum.tile([P, N], BF16, tag="bank")
+            for j in range(BANKS):
+                cols = slice(j * BANK, (j + 1) * BANK)
+                nc.tensor.matmul(out=b_bank[:, cols], lhsT=ones[:], rhs=b_row[:, cols], start=True, stop=True)
+            bank_of["b"] = b_bank
+
+        def ball(engine="V"):
+            if engine == "V":
+                nc.vector.tensor_copy(out=b_all[:], in_=bank_of["b"][:])
+            else:
+                nc.scalar.copy(out=b_all[:], in_=bank_of["b"][:])
+
+        def gsT():
+            flipped = psum.tile([P, P], BF16, tag="bank")
+            nc.tensor.transpose(out=flipped[:], in_=gain_shift_rows[:], identity=identity_bf[:])
+            bank_of["gs"] = flipped
+
+        def gscp():
+            nc.scalar.copy(out=gain_shift[:], in_=bank_of["gs"][:, 0 : 2 * FEATURE_BLOCKS])
+
+        def flipT(i):
             h_words = h_sb[i][:].bitcast(F32)
             flipped = psum.tile([P, PASSES, 2, P], F32, tag="bank")
             for g in range(PASSES):
@@ -130,172 +169,193 @@ def tile_dcadecoderblock_pb_kernel(
                         in_=h_words[:, g * WORDS + u : (g + 1) * WORDS : 2],
                         identity=identity[:],
                     )
-            grouped = rows.tile([P, PASSES * P * PACK], BF16, align_bytes=64)
+            bank_of[("f", i)] = flipped
+
+        def cp(i):
             nc.scalar.copy(
-                out=grouped[:].bitcast(F32).rearrange("p (g r u) -> p g r u", g=PASSES, u=2),
-                in_=flipped[:].rearrange("p g u r -> p g r u"),
+                out=grouped[i][:].bitcast(F32).rearrange("p (g r u) -> p g r u", g=PASSES, u=2),
+                in_=bank_of[("f", i)][:].rearrange("p g u r -> p g r u"),
             )
-            return grouped
 
-        def quantise(i, grouped):
+        def q(i):
             nc.vector.quantize_mx(
-                out=h_codes[:, i, :].bitcast(FP8X4), scales=h_scales[:, i, :], in_=grouped[:]
+                out=h_codes[:, i, :].bitcast(FP8X4), scales=h_scales[:, i, :], in_=grouped[i][:]
             )
 
-        def project(i):
-            banks = []
-            for j in range(BANKS):
-                acc = psum.tile([P, BANK], F32, tag="bank")
-                for g in range(PASSES):
-                    nc.tensor.matmul_mx(
-                        out=acc[:],
-                        lhsT=h_codes[:, i, g * P : (g + 1) * P].bitcast(FP8X4),
-                        lhsT_scale=h_scales[:, i, g * P : (g + 1) * P],
-                        rhs=w_words[:, g, 2 * j * BANK : 2 * (j + 1) * BANK].bitcast(FP4X4),
-                        rhs_scale=w_scales[:, g, j * BANK : (j + 1) * BANK],
-                        start=(g == 0),
-                        stop=(g == PASSES - 1),
-                    )
-                banks.append(acc)
-            return banks
-
-        def add_bias(i, banks):
-            for j in range(BANKS):
-                cols = slice(j * BANK, (j + 1) * BANK)
-                nc.vector.scalar_tensor_tensor(
-                    out=o_sb[i][:, cols],
-                    in0=banks[j][:],
-                    scalar=1.0,
-                    in1=b_all[:, cols],
-                    op0=ALU.mult,
-                    op1=ALU.add,
-                    accum_out=row_sum[i][:, j : j + 1],
+        def mxj(i, j):
+            acc = psum.tile([P, BANK], F32, tag="bank")
+            for g in range(PASSES):
+                nc.tensor.matmul_mx(
+                    out=acc[:],
+                    lhsT=h_codes[:, i, g * P : (g + 1) * P].bitcast(FP8X4),
+                    lhsT_scale=h_scales[:, i, g * P : (g + 1) * P],
+                    rhs=w_words[:, g, 2 * j * BANK : 2 * (j + 1) * BANK].bitcast(FP4X4),
+                    rhs_scale=w_scales[:, g, j * BANK : (j + 1) * BANK],
+                    start=(g == 0),
+                    stop=(g == PASSES - 1),
                 )
-            nc.gpsimd.tensor_scalar(
-                out=neg_mean[i][:],
-                in0=row_sum[i][:, 0:1],
-                scalar1=row_sum[i][:, 1:2],
-                scalar2=-1.0 / N,
-                op0=ALU.add,
-                op1=ALU.mult,
-            )
+            bank_of[("a", i, j)] = acc
 
-        def deviation(i):
-            squares = rows.tile([P, N], BF16)
-            sum_squares = small.tile([P, 1], F32)
-            nc.scalar.activation(
-                out=squares[:], in_=o_sb[i][:], func=ACT.Square, bias=neg_mean[i][:], accum_out=sum_squares[:]
-            )
-            nc.scalar.activation(
-                out=rstd[i][:], in_=sum_squares[:], func=ACT.Abs_reciprocal_sqrt, scale=1.0 / N, bias=eps[:]
-            )
-
-        def normalise(i):
-            if i in VECTOR_NORMALISES:
-                for j in range(BANKS):
-                    cols = slice(j * BANK, (j + 1) * BANK)
-                    nc.vector.tensor_scalar(
-                        out=y_sb[i][:, cols],
-                        in0=o_sb[i][:, cols],
-                        scalar1=neg_mean[i][:],
-                        scalar2=rstd[i][:],
-                        op0=ALU.add,
-                        op1=ALU.mult,
-                    )
-                return
-            neg_mean_over_std = small.tile([P, 1], F32)
-            nc.gpsimd.tensor_scalar(
-                out=neg_mean_over_std[:],
-                in0=neg_mean[i][:],
-                scalar1=rstd[i][:],
-                scalar2=0.0,
+        def v1j(i, j):
+            cols = slice(j * BANK, (j + 1) * BANK)
+            nc.vector.scalar_tensor_tensor(
+                out=o_sb[i][:, cols],
+                in0=bank_of[("a", i, j)][:],
+                scalar=1.0,
+                in1=b_all[:, cols],
                 op0=ALU.mult,
                 op1=ALU.add,
+                accum_out=row_sum[i][:, j : j + 1],
             )
-            for j in range(BANKS):
-                cols = slice(j * BANK, (j + 1) * BANK)
-                nc.gpsimd.tensor_scalar(
-                    out=y_sb[i][:, cols],
-                    in0=o_sb[i][:, cols],
-                    scalar1=rstd[i][:],
-                    scalar2=neg_mean_over_std[:],
-                    op0=ALU.mult,
-                    op1=ALU.add,
+
+        def nm(i, engine="S"):
+            if engine == "S":
+                nc.scalar.activation(
+                    out=mean_junk[i][:], in_=row_sum[i][:], func=ACT.Identity, scale=-1.0 / N, accum_out=neg_mean[i][:]
+                )
+            else:
+                nc.vector.tensor_scalar(
+                    out=neg_mean[i][:], in0=row_sum[i][:, 0:1], scalar1=row_sum[i][:, 1:2], scalar2=-1.0 / N,
+                    op0=ALU.add, op1=ALU.mult,
                 )
 
-        def scale_shift(i, j):
+        def dev(i):
+            nc.scalar.activation(
+                out=squares[i][:], in_=o_sb[i][:], func=ACT.Square, bias=neg_mean[i][:], accum_out=sum_squares[i][:]
+            )
+            nc.scalar.activation(
+                out=rstd[i][:], in_=sum_squares[i][:], func=ACT.Abs_reciprocal_sqrt, scale=1.0 / N, bias=eps[:]
+            )
+
+        def yj(i, j, engine="V"):
+            cols = slice(j * BANK, (j + 1) * BANK)
+            if engine == "V":
+                nc.vector.tensor_scalar(
+                    out=y_sb[i][:, cols], in0=o_sb[i][:, cols], scalar1=neg_mean[i][:], scalar2=rstd[i][:],
+                    op0=ALU.add, op1=ALU.mult,
+                )
+                return
+            if j == 0:
+                nc.gpsimd.tensor_scalar(
+                    out=neg_mean_over_std[i][:], in0=neg_mean[i][:], scalar1=rstd[i][:], scalar2=0.0,
+                    op0=ALU.mult, op1=ALU.add,
+                )
+            nc.gpsimd.tensor_scalar(
+                out=y_sb[i][:, cols], in0=o_sb[i][:, cols], scalar1=rstd[i][:], scalar2=neg_mean_over_std[i][:],
+                op0=ALU.mult, op1=ALU.add,
+            )
+
+        def fwd(i, j):
             y_t = psum.tile([P, BLOCKS_PER_BANK, P], F32, tag="bank")
             for m in range(BLOCKS_PER_BANK):
                 f = j * BLOCKS_PER_BANK + m
                 nc.tensor.transpose(out=y_t[:, m, :], in_=y_sb[i][:, f * P : (f + 1) * P], identity=identity[:])
+            bank_of[("y", i, j)] = y_t
+
+        def zt(i, j, engine="S"):
+            y_t = bank_of[("y", i, j)]
             for m in range(BLOCKS_PER_BANK):
                 f = j * BLOCKS_PER_BANK + m
                 gain = gain_shift[:, f : f + 1]
                 shift = gain_shift[:, FEATURE_BLOCKS + f : FEATURE_BLOCKS + f + 1]
-                if (i, j) in VECTOR_HALVES:
+                if engine == "V":
                     nc.vector.tensor_scalar(
                         out=z_t[i][:, f, :], in0=y_t[:, m, :], scalar1=gain, scalar2=shift, op0=ALU.mult, op1=ALU.add
                     )
                 else:
                     nc.scalar.activation(out=z_t[i][:, f, :], in_=y_t[:, m, :], func=ACT.Identity, scale=gain, bias=shift)
 
-        def finish(i, j):
+        def back(i, j):
             z = psum.tile([P, BANK], F32, tag="bank")
             for m in range(BLOCKS_PER_BANK):
                 nc.tensor.transpose(
                     out=z[:, m * P : (m + 1) * P], in_=z_t[i][:, j * BLOCKS_PER_BANK + m, :], identity=identity[:]
                 )
+            bank_of[("z", i, j)] = z
+
+        def add(i, j):
             cols = slice(j * BANK, (j + 1) * BANK)
-            nc.vector.tensor_tensor(out=result[i][:, cols], in0=z[:], in1=x_sb[:, i, cols], op=ALU.add)
+            nc.vector.tensor_tensor(out=result[i][:, cols], in0=bank_of[("z", i, j)][:], in1=x_sb[:, i, cols], op=ALU.add)
             nc.sync.dma_start(out=out_tiles[i][:, cols], in_=result[i][:, cols])
 
-        grouped = {}
-        banks = {}
-        grouped[0] = flip(0)
-        b_bank = psum.tile([P, N], BF16, tag="bank")
-        for j in range(BANKS):
-            cols = slice(j * BANK, (j + 1) * BANK)
-            nc.tensor.matmul(out=b_bank[:, cols], lhsT=ones[:], rhs=b_row[:, cols], start=True, stop=True)
-        gain_shift_flipped = psum.tile([P, P], BF16, tag="bank")
-        nc.tensor.transpose(out=gain_shift_flipped[:], in_=gain_shift_rows[:], identity=identity_bf[:])
-        nc.scalar.copy(out=gain_shift[:], in_=gain_shift_flipped[:, 0 : 2 * FEATURE_BLOCKS])
-        quantise(0, grouped[0])
-        nc.vector.tensor_copy(out=b_all[:], in_=b_bank[:])
-        grouped[1] = flip(1)
-        banks[0] = project(0)
-        quantise(1, grouped[1])
-        grouped[2] = flip(2)
-        grouped[3] = flip(3)
-        add_bias(0, banks[0])
-        banks[1] = project(1)
-        quantise(2, grouped[2])
-        quantise(3, grouped[3])
-        deviation(0)
-        add_bias(1, banks[1])
-        banks[2] = project(2)
-        banks[3] = project(3)
-        deviation(1)
-        add_bias(2, banks[2])
-        normalise(0)
-        deviation(2)
-        add_bias(3, banks[3])
-        deviation(3)
-        scale_shift(0, 0)
-        scale_shift(0, 1)
-        normalise(1)
-        finish(0, 0)
-        finish(0, 1)
-        normalise(3)
-        scale_shift(1, 0)
-        scale_shift(1, 1)
-        normalise(2)
-        scale_shift(3, 0)
-        scale_shift(3, 1)
-        finish(1, 0)
-        finish(1, 1)
-        finish(3, 0)
-        finish(3, 1)
-        scale_shift(2, 0)
-        scale_shift(2, 1)
-        finish(2, 0)
-        finish(2, 1)
+        clock()
+        flipT(0)
+        cp(0)
+        spread()
+        q(0)
+        ball()
+        gsT()
+        gscp()
+        flipT(1)
+        cp(1)
+        mxj(0, 0)
+        mxj(0, 1)
+        flipT(2)
+        cp(2)
+        flipT(3)
+        cp(3)
+        v1j(0, 0)
+        q(1)
+        v1j(0, 1)
+        nm(0)
+        mxj(1, 0)
+        mxj(1, 1)
+        q(2)
+        dev(0)
+        v1j(1, 0)
+        q(3)
+        v1j(1, 1)
+        nm(1)
+        mxj(2, 0)
+        mxj(2, 1)
+        mxj(3, 0)
+        mxj(3, 1)
+        yj(0, 0, "G")
+        yj(0, 1, "G")
+        dev(1)
+        v1j(2, 0)
+        v1j(2, 1)
+        nm(2)
+        fwd(0, 0)
+        fwd(0, 1)
+        yj(1, 0, "G")
+        yj(1, 1, "G")
+        dev(2)
+        v1j(3, 0)
+        v1j(3, 1)
+        nm(3)
+        dev(3)
+        zt(0, 0, "V")
+        zt(0, 1, "V")
+        back(0, 0)
+        back(0, 1)
+        fwd(1, 0)
+        fwd(1, 1)
+        zt(1, 0)
+        zt(1, 1)
+        yj(2, 0)
+        yj(2, 1)
+        add(0, 0)
+        add(0, 1)
+        fwd(2, 0)
+        fwd(2, 1)
+        back(1, 0)
+        back(1, 1)
+        yj(3, 0)
+        yj(3, 1)
+        zt(2, 0)
+        zt(2, 1)
+        fwd(3, 0)
+        fwd(3, 1)
+        add(1, 0)
+        add(1, 1)
+        back(2, 0)
+        back(2, 1)
+        zt(3, 0)
+        zt(3, 1)
+        add(2, 0)
+        add(2, 1)
+        back(3, 0)
+        back(3, 1)
+        add(3, 0)
+        add(3, 1)

@@ -109,7 +109,8 @@ def tile_dcadecoderblock_pb_kernel(
         make_identity(nc, identity[:])
         make_identity(nc, identity_bf[:])
 
-        nc.sync.dma_start(out=h_sb[0][:], in_=h_tiles[0])
+        for g in range(PASSES):
+            nc.sync.dma_start(out=h_sb[0][:, g * K_PASS : (g + 1) * K_PASS], in_=h_tiles[0][:, g * K_PASS : (g + 1) * K_PASS])
         nc.scalar.dma_start(out=b_row[0:1, :], in_=attn_out_b.unsqueeze(0))
         nc.scalar.dma_start(
             out=gain_shift_rows[0:FEATURE_BLOCKS, :], in_=attn_norm_g.rearrange("(f p) -> f p", p=P)
@@ -119,6 +120,7 @@ def tile_dcadecoderblock_pb_kernel(
             in_=attn_norm_b.rearrange("(f p) -> f p", p=P),
         )
         nc.scalar.activation(out=table_warm[:], in_=eps[:], func=ACT.Abs_reciprocal_sqrt)
+        nc.sync.dma_start(out=h_sb[1][:], in_=h_tiles[1])
         for q in range(4):
             nc.sync.dma_start(
                 out=w_scales[32 * q : 32 * q + 4, :, :].bitcast(I32),
@@ -128,7 +130,6 @@ def tile_dcadecoderblock_pb_kernel(
             out=w_words[:].bitcast(I32),
             in_=attn_out_W_words.rearrange("g p b -> p g b").bitcast(I32),
         )
-        nc.sync.dma_start(out=h_sb[1][:], in_=h_tiles[1])
         nc.sync.dma_start(out=h_sb[2][:], in_=h_tiles[2])
         nc.sync.dma_start(out=h_sb[3][:], in_=h_tiles[3])
         nc.sync.dma_start(out=x_sb[:], in_=x.flatten_outer_dims().rearrange("(i p) n -> p i n", p=P))
@@ -170,6 +171,44 @@ def tile_dcadecoderblock_pb_kernel(
                         identity=identity[:],
                     )
             bank_of[("f", i)] = flipped
+
+        def flipTg(i, g):
+            h_words = h_sb[i][:].bitcast(F32)
+            flipped = psum.tile([P, 2, P], F32, tag="bank")
+            for u in range(2):
+                nc.tensor.transpose(
+                    out=flipped[:, u, :],
+                    in_=h_words[:, g * WORDS + u : (g + 1) * WORDS : 2],
+                    identity=identity[:],
+                )
+            bank_of[("f", i, g)] = flipped
+
+        def cpg(i, g):
+            nc.scalar.copy(
+                out=grouped[i][:, g * K_PASS : (g + 1) * K_PASS].bitcast(F32).rearrange("p (r u) -> p r u", u=2),
+                in_=bank_of[("f", i, g)][:].rearrange("p u r -> p r u"),
+            )
+
+        def qg(i, g):
+            nc.vector.quantize_mx(
+                out=h_codes[:, i, g * P : (g + 1) * P].bitcast(FP8X4),
+                scales=h_scales[:, i, g * P : (g + 1) * P],
+                in_=grouped[i][:, g * K_PASS : (g + 1) * K_PASS],
+            )
+
+        def mxg(i, j, g):
+            if g == 0:
+                acc = psum.tile([P, BANK], F32, tag="bank")
+                bank_of[("a", i, j)] = acc
+            nc.tensor.matmul_mx(
+                out=bank_of[("a", i, j)][:],
+                lhsT=h_codes[:, i, g * P : (g + 1) * P].bitcast(FP8X4),
+                lhsT_scale=h_scales[:, i, g * P : (g + 1) * P],
+                rhs=w_words[:, g, 2 * j * BANK : 2 * (j + 1) * BANK].bitcast(FP4X4),
+                rhs_scale=w_scales[:, g, j * BANK : (j + 1) * BANK],
+                start=(g == 0),
+                stop=(g == PASSES - 1),
+            )
 
         def cp(i):
             nc.scalar.copy(
@@ -279,17 +318,22 @@ def tile_dcadecoderblock_pb_kernel(
             nc.sync.dma_start(out=out_tiles[i][:, cols], in_=result[i][:, cols])
 
         clock()
-        flipT(0)
-        cp(0)
+        flipTg(0, 0)
+        cpg(0, 0)
+        flipTg(0, 1)
+        cpg(0, 1)
         spread()
-        q(0)
+        qg(0, 0)
+        qg(0, 1)
         ball()
-        gsT()
-        gscp()
         flipT(1)
         cp(1)
-        mxj(0, 0)
-        mxj(0, 1)
+        gsT()
+        gscp()
+        mxg(0, 0, 0)
+        mxg(0, 1, 0)
+        mxg(0, 0, 1)
+        mxg(0, 1, 1)
         flipT(2)
         cp(2)
         flipT(3)
@@ -297,56 +341,56 @@ def tile_dcadecoderblock_pb_kernel(
         v1j(0, 0)
         q(1)
         v1j(0, 1)
-        nm(0)
         mxj(1, 0)
         mxj(1, 1)
         q(2)
+        nm(0, "V")
         dev(0)
         v1j(1, 0)
         q(3)
         v1j(1, 1)
-        nm(1)
         mxj(2, 0)
         mxj(2, 1)
         mxj(3, 0)
         mxj(3, 1)
         yj(0, 0, "G")
         yj(0, 1, "G")
-        dev(1)
         v1j(2, 0)
+        nm(1, "V")
+        dev(1)
         v1j(2, 1)
-        nm(2)
         fwd(0, 0)
         fwd(0, 1)
-        yj(1, 0, "G")
-        yj(1, 1, "G")
-        dev(2)
         v1j(3, 0)
+        nm(2, "V")
+        dev(2)
         v1j(3, 1)
-        nm(3)
+        nm(3, "V")
         dev(3)
+        yj(1, 0)
+        yj(1, 1)
         zt(0, 0, "V")
+        fwd(1, 0)
+        fwd(1, 1)
         zt(0, 1, "V")
         back(0, 0)
         back(0, 1)
-        fwd(1, 0)
-        fwd(1, 1)
-        zt(1, 0)
-        zt(1, 1)
         yj(2, 0)
         yj(2, 1)
-        add(0, 0)
-        add(0, 1)
+        zt(1, 0)
+        zt(1, 1)
         fwd(2, 0)
         fwd(2, 1)
-        back(1, 0)
-        back(1, 1)
+        add(0, 0)
         yj(3, 0)
         yj(3, 1)
-        zt(2, 0)
-        zt(2, 1)
+        add(0, 1)
+        back(1, 0)
+        back(1, 1)
         fwd(3, 0)
         fwd(3, 1)
+        zt(2, 0)
+        zt(2, 1)
         add(1, 0)
         add(1, 1)
         back(2, 0)

@@ -83,7 +83,6 @@ def tile_dcadecoderblock_pb_kernel(
         neg_mean = []
         sum_squares = []
         rstd = []
-        neg_mean_over_std = []
         for i in range(TOKEN_TILES):
             h_sb.append(rows.tile([P, K], BF16, name="h_sb"))
             grouped.append(rows.tile([P, PASSES * P * PACK], BF16, name="grouped", align_bytes=64))
@@ -97,7 +96,6 @@ def tile_dcadecoderblock_pb_kernel(
             neg_mean.append(small.tile([P, 1], F32, name="neg_mean"))
             sum_squares.append(small.tile([P, 1], F32, name="sum_squares"))
             rstd.append(small.tile([P, 1], F32, name="rstd"))
-            neg_mean_over_std.append(small.tile([P, 1], F32, name="neg_mean_over_std"))
         bank_of = {}
 
         nc.gpsimd.memset(w_scales[:].rearrange("p g n -> p (g n)").bitcast(F32), 0.0)
@@ -120,12 +118,12 @@ def tile_dcadecoderblock_pb_kernel(
             in_=attn_norm_b.rearrange("(f p) -> f p", p=P),
         )
         nc.scalar.activation(out=table_warm[:], in_=eps[:], func=ACT.Abs_reciprocal_sqrt)
-        nc.sync.dma_start(out=h_sb[1][:], in_=h_tiles[1])
         for q in range(4):
             nc.sync.dma_start(
                 out=w_scales[32 * q : 32 * q + 4, :, :].bitcast(I32),
                 in_=attn_out_W_scales[:, 4 * q : 4 * q + 4, :].rearrange("g r n -> r g n").bitcast(I32),
             )
+        nc.sync.dma_start(out=h_sb[1][:], in_=h_tiles[1])
         nc.sync.dma_start(
             out=w_words[:].bitcast(I32),
             in_=attn_out_W_words.rearrange("g p b -> p g b").bitcast(I32),
@@ -254,8 +252,8 @@ def tile_dcadecoderblock_pb_kernel(
                 )
             else:
                 nc.vector.tensor_scalar(
-                    out=neg_mean[i][:], in0=row_sum[i][:, 0:1], scalar1=row_sum[i][:, 1:2], scalar2=-1.0 / N,
-                    op0=ALU.add, op1=ALU.mult,
+                    out=mean_junk[i][:], in0=row_sum[i][:], scalar1=-1.0 / N, scalar2=None,
+                    op0=ALU.mult, op1=ALU.add, accum_out=neg_mean[i][:],
                 )
 
         def dev(i):
@@ -274,14 +272,9 @@ def tile_dcadecoderblock_pb_kernel(
                     op0=ALU.add, op1=ALU.mult,
                 )
                 return
-            if j == 0:
-                nc.gpsimd.tensor_scalar(
-                    out=neg_mean_over_std[i][:], in0=neg_mean[i][:], scalar1=rstd[i][:], scalar2=0.0,
-                    op0=ALU.mult, op1=ALU.add,
-                )
             nc.gpsimd.tensor_scalar(
-                out=y_sb[i][:, cols], in0=o_sb[i][:, cols], scalar1=rstd[i][:], scalar2=neg_mean_over_std[i][:],
-                op0=ALU.mult, op1=ALU.add,
+                out=y_sb[i][:, cols], in0=o_sb[i][:, cols], scalar1=neg_mean[i][:], scalar2=rstd[i][:],
+                op0=ALU.add, op1=ALU.mult,
             )
 
         def fwd(i, j):

@@ -28,6 +28,7 @@ EPS = 1e-5
 FEATURE_BLOCKS = N // P
 BLOCKS_PER_BANK = BANK // P
 PSUM_BANKS = 8
+WORK_BANKS = PSUM_BANKS - 1
 
 CLOCK_WARM_MATMULS = 2
 
@@ -53,7 +54,8 @@ def tile_dcadecoderblock_pb_kernel(
         keep = ctx.enter_context(tc.tile_pool(name="keep", bufs=1))
         rows = ctx.enter_context(tc.tile_pool(name="rows", bufs=TOKEN_TILES))
         small = ctx.enter_context(tc.tile_pool(name="small", bufs=TOKEN_TILES))
-        psum = ctx.enter_context(tc.psum_pool(name="psum", bufs=PSUM_BANKS))
+        psum = ctx.enter_context(tc.psum_pool(name="psum", bufs=WORK_BANKS))
+        psum_clock = ctx.enter_context(tc.psum_pool(name="psum_clock", bufs=1))
         ctx.enter_context(tc.manual_schedule())
 
         w_words = keep.tile([P, PASSES, 2 * N], U8, align_bytes=64)
@@ -132,10 +134,14 @@ def tile_dcadecoderblock_pb_kernel(
         nc.sync.dma_start(out=h_sb[3][:], in_=h_tiles[3])
         nc.sync.dma_start(out=x_sb[:], in_=x.flatten_outer_dims().rearrange("(i p) n -> p i n", p=P))
 
+        clock_bank = psum_clock.tile([P, BANK], F32)
+
         def clock():
-            clock_bank = psum.tile([P, BANK], F32, tag="bank")
             for r in range(CLOCK_WARM_MATMULS):
                 nc.tensor.matmul(out=clock_bank[:], lhsT=ones[:], rhs=clock_warm[:], start=True, stop=True)
+
+        def wm():
+            nc.tensor.matmul(out=clock_bank[:, 0:P], lhsT=identity[:], rhs=identity[:], start=True, stop=True)
 
         def spread():
             b_bank = psum.tile([P, N], BF16, tag="bank")
@@ -346,6 +352,7 @@ def tile_dcadecoderblock_pb_kernel(
         mxj(2, 1)
         mxj(3, 0)
         mxj(3, 1)
+        wm()
         yj(0, 0, "G")
         yj(0, 1, "G")
         v1j(2, 0)
@@ -353,7 +360,10 @@ def tile_dcadecoderblock_pb_kernel(
         dev(1)
         v1j(2, 1)
         fwd(0, 0)
+        wm()
         fwd(0, 1)
+        wm()
+        wm()
         v1j(3, 0)
         nm(2, "V")
         dev(2)
@@ -368,6 +378,7 @@ def tile_dcadecoderblock_pb_kernel(
         zt(0, 1, "V")
         back(0, 0)
         back(0, 1)
+        wm()
         yj(2, 0)
         yj(2, 1)
         zt(1, 0)
@@ -380,6 +391,7 @@ def tile_dcadecoderblock_pb_kernel(
         add(0, 1)
         back(1, 0)
         back(1, 1)
+        wm()
         fwd(3, 0)
         fwd(3, 1)
         zt(2, 0)

@@ -58,7 +58,9 @@ def tile_dcadecoderblock_pb_kernel(
         psum_clock = ctx.enter_context(tc.psum_pool(name="psum_clock", bufs=1))
         ctx.enter_context(tc.manual_schedule())
 
-        w_words = keep.tile([P, PASSES, 2 * N], U8, align_bytes=64)
+        w_words = []
+        for j in range(BANKS):
+            w_words.append(keep.tile([P, PASSES, 2 * BANK], U8, name="w_words_%d" % j, align_bytes=64))
         w_scales = keep.tile([P, PASSES, N], U8, align_bytes=64)
         h_codes = keep.tile([P, TOKEN_TILES, PASSES * P], U32, align_bytes=64)
         h_scales = keep.tile([P, TOKEN_TILES, PASSES * P], U8, align_bytes=64)
@@ -101,17 +103,17 @@ def tile_dcadecoderblock_pb_kernel(
         bank_of = {}
 
         nc.gpsimd.memset(w_scales[:].rearrange("p g n -> p (g n)").bitcast(F32), 0.0)
+        nc.vector.memset(eps[:], EPS)
+        nc.vector.memset(b_row[:].bitcast(I32), 0)
         nc.vector.memset(ones[:], 1.0)
         nc.vector.memset(clock_warm[:].bitcast(I32), 0)
-        nc.vector.memset(b_row[:].bitcast(I32), 0)
         nc.vector.memset(gain_shift_rows[:].bitcast(I32), 0)
-        nc.vector.memset(eps[:], EPS)
         make_identity(nc, identity[:])
         make_identity(nc, identity_bf[:])
 
         for g in range(PASSES):
             nc.sync.dma_start(out=h_sb[0][:, g * K_PASS : (g + 1) * K_PASS], in_=h_tiles[0][:, g * K_PASS : (g + 1) * K_PASS])
-        nc.scalar.dma_start(out=b_row[0:1, :], in_=attn_out_b.unsqueeze(0))
+        nc.scalar.activation(out=table_warm[:], in_=eps[:], func=ACT.Abs_reciprocal_sqrt)
         nc.scalar.dma_start(
             out=gain_shift_rows[0:FEATURE_BLOCKS, :], in_=attn_norm_g.rearrange("(f p) -> f p", p=P)
         )
@@ -119,16 +121,20 @@ def tile_dcadecoderblock_pb_kernel(
             out=gain_shift_rows[FEATURE_BLOCKS : 2 * FEATURE_BLOCKS, :],
             in_=attn_norm_b.rearrange("(f p) -> f p", p=P),
         )
-        nc.scalar.activation(out=table_warm[:], in_=eps[:], func=ACT.Abs_reciprocal_sqrt)
         for q in range(4):
             nc.sync.dma_start(
                 out=w_scales[32 * q : 32 * q + 4, :, :].bitcast(I32),
                 in_=attn_out_W_scales[:, 4 * q : 4 * q + 4, :].rearrange("g r n -> r g n").bitcast(I32),
             )
+        nc.sync.dma_start(out=b_row[0:1, :], in_=attn_out_b.unsqueeze(0))
+        nc.sync.dma_start(
+            out=w_words[0][:].bitcast(I32),
+            in_=attn_out_W_words.rearrange("g p b -> p g b")[:, :, 0 * 2 * BANK : 1 * 2 * BANK].bitcast(I32),
+        )
         nc.sync.dma_start(out=h_sb[1][:], in_=h_tiles[1])
         nc.sync.dma_start(
-            out=w_words[:].bitcast(I32),
-            in_=attn_out_W_words.rearrange("g p b -> p g b").bitcast(I32),
+            out=w_words[1][:].bitcast(I32),
+            in_=attn_out_W_words.rearrange("g p b -> p g b")[:, :, 1 * 2 * BANK : 2 * 2 * BANK].bitcast(I32),
         )
         nc.sync.dma_start(out=h_sb[2][:], in_=h_tiles[2])
         nc.sync.dma_start(out=h_sb[3][:], in_=h_tiles[3])
@@ -208,7 +214,7 @@ def tile_dcadecoderblock_pb_kernel(
                 out=bank_of[("a", i, j)][:],
                 lhsT=h_codes[:, i, g * P : (g + 1) * P].bitcast(FP8X4),
                 lhsT_scale=h_scales[:, i, g * P : (g + 1) * P],
-                rhs=w_words[:, g, 2 * j * BANK : 2 * (j + 1) * BANK].bitcast(FP4X4),
+                rhs=w_words[j][:, g, :].bitcast(FP4X4),
                 rhs_scale=w_scales[:, g, j * BANK : (j + 1) * BANK],
                 start=(g == 0),
                 stop=(g == PASSES - 1),
@@ -232,7 +238,7 @@ def tile_dcadecoderblock_pb_kernel(
                     out=acc[:],
                     lhsT=h_codes[:, i, g * P : (g + 1) * P].bitcast(FP8X4),
                     lhsT_scale=h_scales[:, i, g * P : (g + 1) * P],
-                    rhs=w_words[:, g, 2 * j * BANK : 2 * (j + 1) * BANK].bitcast(FP4X4),
+                    rhs=w_words[j][:, g, :].bitcast(FP4X4),
                     rhs_scale=w_scales[:, g, j * BANK : (j + 1) * BANK],
                     start=(g == 0),
                     stop=(g == PASSES - 1),
@@ -330,8 +336,8 @@ def tile_dcadecoderblock_pb_kernel(
         gsT()
         gscp()
         mxg(0, 0, 0)
-        mxg(0, 1, 0)
         mxg(0, 0, 1)
+        mxg(0, 1, 0)
         mxg(0, 1, 1)
         flipT(2)
         cp(2)

@@ -114,30 +114,30 @@ def tile_dcadecoderblock_pb_kernel(
         for g in range(PASSES):
             nc.sync.dma_start(out=h_sb[0][:, g * K_PASS : (g + 1) * K_PASS], in_=h_tiles[0][:, g * K_PASS : (g + 1) * K_PASS])
         nc.scalar.activation(out=table_warm[:], in_=eps[:], func=ACT.Abs_reciprocal_sqrt)
-        nc.scalar.dma_start(
-            out=gain_shift_rows[0:FEATURE_BLOCKS, :], in_=attn_norm_g.rearrange("(f p) -> f p", p=P)
-        )
-        nc.scalar.dma_start(
-            out=gain_shift_rows[FEATURE_BLOCKS : 2 * FEATURE_BLOCKS, :],
-            in_=attn_norm_b.rearrange("(f p) -> f p", p=P),
-        )
         for q in range(4):
             nc.sync.dma_start(
                 out=w_scales[32 * q : 32 * q + 4, :, :].bitcast(I32),
                 in_=attn_out_W_scales[:, 4 * q : 4 * q + 4, :].rearrange("g r n -> r g n").bitcast(I32),
             )
-        nc.sync.dma_start(out=b_row[0:1, :], in_=attn_out_b.unsqueeze(0))
         nc.sync.dma_start(
             out=w_words[0][:].bitcast(I32),
             in_=attn_out_W_words.rearrange("g p b -> p g b")[:, :, 0 * 2 * BANK : 1 * 2 * BANK].bitcast(I32),
         )
         nc.sync.dma_start(out=h_sb[1][:], in_=h_tiles[1])
+        nc.sync.dma_start(out=b_row[0:1, :], in_=attn_out_b.unsqueeze(0))
         nc.sync.dma_start(
             out=w_words[1][:].bitcast(I32),
             in_=attn_out_W_words.rearrange("g p b -> p g b")[:, :, 1 * 2 * BANK : 2 * 2 * BANK].bitcast(I32),
         )
         nc.sync.dma_start(out=h_sb[2][:], in_=h_tiles[2])
         nc.sync.dma_start(out=h_sb[3][:], in_=h_tiles[3])
+        nc.sync.dma_start(
+            out=gain_shift_rows[0:FEATURE_BLOCKS, :], in_=attn_norm_g.rearrange("(f p) -> f p", p=P)
+        )
+        nc.sync.dma_start(
+            out=gain_shift_rows[FEATURE_BLOCKS : 2 * FEATURE_BLOCKS, :],
+            in_=attn_norm_b.rearrange("(f p) -> f p", p=P),
+        )
         nc.sync.dma_start(out=x_sb[:], in_=x.flatten_outer_dims().rearrange("(i p) n -> p i n", p=P))
 
         clock_bank = psum_clock.tile([P, BANK], F32)
@@ -327,20 +327,20 @@ def tile_dcadecoderblock_pb_kernel(
         cpg(0, 0)
         flipTg(0, 1)
         cpg(0, 1)
-        spread()
         qg(0, 0)
         qg(0, 1)
-        ball()
-        flipT(1)
-        cp(1)
-        gsT()
-        gscp()
         mxg(0, 0, 0)
         mxg(0, 0, 1)
+        flipT(1)
+        cp(1)
+        spread()
+        ball()
         mxg(0, 1, 0)
         mxg(0, 1, 1)
         flipT(2)
         cp(2)
+        gsT()
+        gscp()
         flipT(3)
         cp(3)
         v1j(0, 0)

@@ -30,7 +30,7 @@ BLOCKS_PER_BANK = BANK // P
 PSUM_BANKS = 8
 WORK_BANKS = PSUM_BANKS - 1
 
-CLOCK_WARM_MATMULS = 2
+CLOCK_WARM_MATMULS = 4
 
 FLOPS = 2 * TOKENS * K * N
 
@@ -102,11 +102,11 @@ def tile_dcadecoderblock_pb_kernel(
             rstd.append(small.tile([P, 1], F32, name="rstd"))
         bank_of = {}
 
-        nc.gpsimd.memset(w_scales[:].rearrange("p g n -> p (g n)").bitcast(F32), 0.0)
-        nc.vector.memset(eps[:], EPS)
-        nc.vector.memset(b_row[:].bitcast(I32), 0)
         nc.vector.memset(ones[:], 1.0)
         nc.vector.memset(clock_warm[:].bitcast(I32), 0)
+        nc.vector.memset(eps[:], EPS)
+        nc.vector.memset(w_scales[:].rearrange("p g n -> p (g n)").bitcast(I32), 0)
+        nc.vector.memset(b_row[:].bitcast(I32), 0)
         nc.vector.memset(gain_shift_rows[:].bitcast(I32), 0)
         make_identity(nc, identity[:])
         make_identity(nc, identity_bf[:])
@@ -358,7 +358,6 @@ def tile_dcadecoderblock_pb_kernel(
         mxj(2, 1)
         mxj(3, 0)
         mxj(3, 1)
-        wm()
         yj(0, 0, "G")
         yj(0, 1, "G")
         v1j(2, 0)
@@ -366,10 +365,7 @@ def tile_dcadecoderblock_pb_kernel(
         dev(1)
         v1j(2, 1)
         fwd(0, 0)
-        wm()
         fwd(0, 1)
-        wm()
-        wm()
         v1j(3, 0)
         nm(2, "V")
         dev(2)
@@ -384,7 +380,6 @@ def tile_dcadecoderblock_pb_kernel(
         zt(0, 1, "V")
         back(0, 0)
         back(0, 1)
-        wm()
         yj(2, 0)
         yj(2, 1)
         zt(1, 0)
@@ -397,7 +392,6 @@ def tile_dcadecoderblock_pb_kernel(
         add(0, 1)
         back(1, 0)
         back(1, 1)
-        wm()
         fwd(3, 0)
         fwd(3, 1)
         zt(2, 0)

@@ -111,9 +111,9 @@ def tile_dcadecoderblock_pb_kernel(
         make_identity(nc, identity[:])
         make_identity(nc, identity_bf[:])
 
-        for g in range(PASSES):
-            nc.sync.dma_start(out=h_sb[0][:, g * K_PASS : (g + 1) * K_PASS], in_=h_tiles[0][:, g * K_PASS : (g + 1) * K_PASS])
+        nc.sync.dma_start(out=h_sb[0][:], in_=h_tiles[0])
         nc.scalar.activation(out=table_warm[:], in_=eps[:], func=ACT.Abs_reciprocal_sqrt)
+        nc.sync.dma_start(out=b_row[0:1, :], in_=attn_out_b.unsqueeze(0))
         for q in range(4):
             nc.sync.dma_start(
                 out=w_scales[32 * q : 32 * q + 4, :, :].bitcast(I32),
@@ -124,7 +124,6 @@ def tile_dcadecoderblock_pb_kernel(
             in_=attn_out_W_words.rearrange("g p b -> p g b")[:, :, 0 * 2 * BANK : 1 * 2 * BANK].bitcast(I32),
         )
         nc.sync.dma_start(out=h_sb[1][:], in_=h_tiles[1])
-        nc.sync.dma_start(out=b_row[0:1, :], in_=attn_out_b.unsqueeze(0))
         nc.sync.dma_start(
             out=w_words[1][:].bitcast(I32),
             in_=attn_out_W_words.rearrange("g p b -> p g b")[:, :, 1 * 2 * BANK : 2 * 2 * BANK].bitcast(I32),
@@ -145,6 +144,15 @@ def tile_dcadecoderblock_pb_kernel(
         def clock():
             for r in range(CLOCK_WARM_MATMULS):
                 nc.tensor.matmul(out=clock_bank[:], lhsT=ones[:], rhs=clock_warm[:], start=True, stop=True)
+
+        def mxk(n=2):
+            for r in range(n):
+                nc.tensor.matmul_mx(
+                    out=clock_bank[:],
+                    lhsT=h_codes[:, 0, 0:P].bitcast(FP8X4), lhsT_scale=h_scales[:, 0, 0:P],
+                    rhs=w_words[0][:, 0, :].bitcast(FP4X4), rhs_scale=w_scales[:, 0, 0:BANK],
+                    start=True, stop=True,
+                )
 
         def wm():
             nc.tensor.matmul(out=clock_bank[:, 0:P], lhsT=identity[:], rhs=identity[:], start=True, stop=True)
@@ -272,6 +280,8 @@ def tile_dcadecoderblock_pb_kernel(
             nc.scalar.activation(
                 out=squares[i][:], in_=o_sb[i][:], func=ACT.Square, bias=neg_mean[i][:], accum_out=sum_squares[i][:]
             )
+
+        def rs(i):
             nc.scalar.activation(
                 out=rstd[i][:], in_=sum_squares[i][:], func=ACT.Abs_reciprocal_sqrt, scale=1.0 / N, bias=eps[:]
             )
@@ -327,22 +337,22 @@ def tile_dcadecoderblock_pb_kernel(
         cpg(0, 0)
         flipTg(0, 1)
         cpg(0, 1)
+        spread()
         qg(0, 0)
         qg(0, 1)
+        ball()
         mxg(0, 0, 0)
         mxg(0, 0, 1)
         flipT(1)
         cp(1)
-        spread()
-        ball()
         mxg(0, 1, 0)
         mxg(0, 1, 1)
         flipT(2)
         cp(2)
-        gsT()
-        gscp()
         flipT(3)
         cp(3)
+        gsT()
+        gscp()
         v1j(0, 0)
         q(1)
         v1j(0, 1)
@@ -351,6 +361,7 @@ def tile_dcadecoderblock_pb_kernel(
         q(2)
         nm(0, "V")
         dev(0)
+        rs(0)
         v1j(1, 0)
         q(3)
         v1j(1, 1)
@@ -363,15 +374,18 @@ def tile_dcadecoderblock_pb_kernel(
         v1j(2, 0)
         nm(1, "V")
         dev(1)
+        rs(1)
         v1j(2, 1)
         fwd(0, 0)
         fwd(0, 1)
         v1j(3, 0)
         nm(2, "V")
         dev(2)
+        rs(2)
         v1j(3, 1)
         nm(3, "V")
         dev(3)
+        rs(3)
         yj(1, 0)
         yj(1, 1)
         zt(0, 0, "V")

@@ -70,7 +70,6 @@ def tile_dcadecoderblock_pb_kernel(
         gain_shift_rows = keep.tile([P, P], BF16)
         gain_shift = keep.tile([P, 2 * FEATURE_BLOCKS], F32)
         ones = keep.tile([P, P], BF16)
-        clock_warm = keep.tile([P, BANK], BF16)
         identity = keep.tile([P, P], F32)
         identity_bf = keep.tile([P, P], BF16)
         eps = keep.tile([P, 1], F32)
@@ -103,7 +102,6 @@ def tile_dcadecoderblock_pb_kernel(
         bank_of = {}
 
         nc.vector.memset(ones[:], 1.0)
-        nc.vector.memset(clock_warm[:].bitcast(I32), 0)
         nc.vector.memset(eps[:], EPS)
         nc.vector.memset(w_scales[:].rearrange("p g n -> p (g n)").bitcast(I32), 0)
         nc.vector.memset(b_row[:].bitcast(I32), 0)
@@ -113,16 +111,16 @@ def tile_dcadecoderblock_pb_kernel(
 
         nc.sync.dma_start(out=h_sb[0][:], in_=h_tiles[0])
         nc.scalar.activation(out=table_warm[:], in_=eps[:], func=ACT.Abs_reciprocal_sqrt)
-        nc.sync.dma_start(out=b_row[0:1, :], in_=attn_out_b.unsqueeze(0))
+        nc.sync.dma_start(
+            out=w_words[0][:].bitcast(I32),
+            in_=attn_out_W_words.rearrange("g p b -> p g b")[:, :, 0 * 2 * BANK : 1 * 2 * BANK].bitcast(I32),
+        )
         for q in range(4):
             nc.sync.dma_start(
                 out=w_scales[32 * q : 32 * q + 4, :, :].bitcast(I32),
                 in_=attn_out_W_scales[:, 4 * q : 4 * q + 4, :].rearrange("g r n -> r g n").bitcast(I32),
             )
-        nc.sync.dma_start(
-            out=w_words[0][:].bitcast(I32),
-            in_=attn_out_W_words.rearrange("g p b -> p g b")[:, :, 0 * 2 * BANK : 1 * 2 * BANK].bitcast(I32),
-        )
+        nc.sync.dma_start(out=b_row[0:1, :], in_=attn_out_b.unsqueeze(0))
         nc.sync.dma_start(out=h_sb[1][:], in_=h_tiles[1])
         nc.sync.dma_start(
             out=w_words[1][:].bitcast(I32),
@@ -143,19 +141,7 @@ def tile_dcadecoderblock_pb_kernel(
 
         def clock():
             for r in range(CLOCK_WARM_MATMULS):
-                nc.tensor.matmul(out=clock_bank[:], lhsT=ones[:], rhs=clock_warm[:], start=True, stop=True)
-
-        def mxk(n=2):
-            for r in range(n):
-                nc.tensor.matmul_mx(
-                    out=clock_bank[:],
-                    lhsT=h_codes[:, 0, 0:P].bitcast(FP8X4), lhsT_scale=h_scales[:, 0, 0:P],
-                    rhs=w_words[0][:, 0, :].bitcast(FP4X4), rhs_scale=w_scales[:, 0, 0:BANK],
-                    start=True, stop=True,
-                )
-
-        def wm():
-            nc.tensor.matmul(out=clock_bank[:, 0:P], lhsT=identity[:], rhs=identity[:], start=True, stop=True)
+                nc.tensor.matmul(out=clock_bank[:], lhsT=ones[:], rhs=ones[:].unsqueeze(1).to_broadcast([P, BLOCKS_PER_BANK, P]), start=True, stop=True)
 
         def spread():
             b_bank = psum.tile([P, N], BF16, tag="bank")
@@ -341,21 +327,21 @@ def tile_dcadecoderblock_pb_kernel(
         qg(0, 0)
         qg(0, 1)
         ball()
-        mxg(0, 0, 0)
-        mxg(0, 0, 1)
         flipT(1)
         cp(1)
+        mxg(0, 0, 0)
+        mxg(0, 0, 1)
         mxg(0, 1, 0)
         mxg(0, 1, 1)
+        v1j(0, 0)
+        q(1)
+        v1j(0, 1)
         flipT(2)
         cp(2)
         flipT(3)
         cp(3)
         gsT()
         gscp()
-        v1j(0, 0)
-        q(1)
-        v1j(0, 1)
         mxj(1, 0)
         mxj(1, 1)
         q(2)
@@ -363,8 +349,9 @@ def tile_dcadecoderblock_pb_kernel(
         dev(0)
         rs(0)
         v1j(1, 0)
-        q(3)
         v1j(1, 1)
+        q(3)
+        nm(1, "V")
         mxj(2, 0)
         mxj(2, 1)
         mxj(3, 0)
@@ -372,45 +359,44 @@ def tile_dcadecoderblock_pb_kernel(
         yj(0, 0, "G")
         yj(0, 1, "G")
         v1j(2, 0)
-        nm(1, "V")
         dev(1)
         rs(1)
         v1j(2, 1)
+        nm(2, "V")
+        yj(1, 0, "G")
+        yj(1, 1, "G")
         fwd(0, 0)
         fwd(0, 1)
         v1j(3, 0)
-        nm(2, "V")
         dev(2)
         rs(2)
         v1j(3, 1)
         nm(3, "V")
+        yj(2, 0, "G")
+        yj(2, 1, "G")
         dev(3)
         rs(3)
-        yj(1, 0)
-        yj(1, 1)
         zt(0, 0, "V")
-        fwd(1, 0)
-        fwd(1, 1)
         zt(0, 1, "V")
+        fwd(1, 0)
         back(0, 0)
+        fwd(1, 1)
         back(0, 1)
-        yj(2, 0)
-        yj(2, 1)
-        zt(1, 0)
+        zt(1, 0, "V")
         zt(1, 1)
-        fwd(2, 0)
-        fwd(2, 1)
         add(0, 0)
         yj(3, 0)
         yj(3, 1)
         add(0, 1)
+        fwd(2, 0)
         back(1, 0)
-        back(1, 1)
-        fwd(3, 0)
-        fwd(3, 1)
+        fwd(2, 1)
         zt(2, 0)
         zt(2, 1)
+        back(1, 1)
         add(1, 0)
+        fwd(3, 0)
+        fwd(3, 1)
         add(1, 1)
         back(2, 0)
         back(2, 1)

@@ -30,7 +30,7 @@ BLOCKS_PER_BANK = BANK // P
 PSUM_BANKS = 8
 WORK_BANKS = PSUM_BANKS - 1
 
-CLOCK_WARM_MATMULS = 4
+CLOCK_WARM_MATMULS = 3
 
 FLOPS = 2 * TOKENS * K * N
 
@@ -142,6 +142,10 @@ def tile_dcadecoderblock_pb_kernel(
         def clock():
             for r in range(CLOCK_WARM_MATMULS):
                 nc.tensor.matmul(out=clock_bank[:], lhsT=ones[:], rhs=ones[:].unsqueeze(1).to_broadcast([P, BLOCKS_PER_BANK, P]), start=True, stop=True)
+
+        def mxk(n=2):
+            for r in range(n):
+                nc.tensor.matmul(out=clock_bank[:, 0:P], lhsT=identity[:], rhs=identity[:], start=True, stop=True)
 
         def spread():
             b_bank = psum.tile([P, N], BF16, tag="bank")
@@ -367,6 +371,7 @@ def tile_dcadecoderblock_pb_kernel(
         yj(1, 1, "G")
         fwd(0, 0)
         fwd(0, 1)
+        mxk()
         v1j(3, 0)
         dev(2)
         rs(2)
@@ -380,6 +385,7 @@ def tile_dcadecoderblock_pb_kernel(
         zt(0, 1, "V")
         fwd(1, 0)
         back(0, 0)
+        mxk()
         fwd(1, 1)
         back(0, 1)
         zt(1, 0, "V")

from contextlib import ExitStack

import concourse.mybir as mybir
from concourse.masks import make_identity

F32 = mybir.dt.float32
BF16 = mybir.dt.bfloat16
I32 = mybir.dt.int32
U32 = mybir.dt.uint32
U8 = mybir.dt.uint8
FP8X4 = mybir.dt.float8_e4m3fn_x4
FP4X4 = mybir.dt.float4_e2m1fn_x4
ALU = mybir.AluOpType
ACT = mybir.ActivationFunctionType

P = 128
PACK = 4
K_PASS = P * PACK
TOKENS = 512
K = 1024
N = 1024
BANK = 512
TOKEN_TILES = TOKENS // P
PASSES = K // K_PASS
BANKS = N // BANK
WORDS = K_PASS // 2
EPS = 1e-5
FEATURE_BLOCKS = N // P
BLOCKS_PER_BANK = BANK // P
PSUM_BANKS = 8
WORK_BANKS = PSUM_BANKS - 1

CLOCK_WARM_MATMULS = 3

FLOPS = 2 * TOKENS * K * N


def tile_dcadecoderblock_pb_kernel(
    tc,
    h_attn,
    x,
    attn_out_W_words,
    attn_out_W_scales,
    attn_out_b,
    attn_norm_g,
    attn_norm_b,
    out,
):
    nc = tc.nc
    h_tiles = h_attn.flatten_outer_dims().rearrange("(i p) k -> i p k", p=P)
    out_tiles = out.flatten_outer_dims().rearrange("(i p) n -> i p n", p=P)

    with ExitStack() as ctx:
        keep = ctx.enter_context(tc.tile_pool(name="keep", bufs=1))
        rows = ctx.enter_context(tc.tile_pool(name="rows", bufs=TOKEN_TILES))
        small = ctx.enter_context(tc.tile_pool(name="small", bufs=TOKEN_TILES))
        psum = ctx.enter_context(tc.psum_pool(name="psum", bufs=WORK_BANKS))
        psum_clock = ctx.enter_context(tc.psum_pool(name="psum_clock", bufs=1))
        ctx.enter_context(tc.manual_schedule())

        w_words = []
        for j in range(BANKS):
            w_words.append(keep.tile([P, PASSES, 2 * BANK], U8, name="w_words_%d" % j, align_bytes=64))
        w_scales = keep.tile([P, PASSES, N], U8, align_bytes=64)
        h_codes = keep.tile([P, TOKEN_TILES, PASSES * P], U32, align_bytes=64)
        h_scales = keep.tile([P, TOKEN_TILES, PASSES * P], U8, align_bytes=64)
        x_sb = keep.tile([P, TOKEN_TILES, N], BF16)
        b_row = keep.tile([P, N], BF16)
        b_all = keep.tile([P, N], BF16)
        gain_shift_rows = keep.tile([P, P], BF16)
        gain_shift = keep.tile([P, 2 * FEATURE_BLOCKS], F32)
        ones = keep.tile([P, P], BF16)
        identity = keep.tile([P, P], F32)
        identity_bf = keep.tile([P, P], BF16)
        eps = keep.tile([P, 1], F32)
        table_warm = keep.tile([P, 1], F32)
        h_sb = []
        grouped = []
        o_sb = []
        y_sb = []
        z_t = []
        result = []
        squares = []
        row_sum = []
        mean_junk = []
        neg_mean = []
        sum_squares = []
        rstd = []
        for i in range(TOKEN_TILES):
            h_sb.append(rows.tile([P, K], BF16, name="h_sb"))
            grouped.append(rows.tile([P, PASSES * P * PACK], BF16, name="grouped", align_bytes=64))
            o_sb.append(rows.tile([P, N], F32, name="o_sb"))
            y_sb.append(rows.tile([P, N], F32, name="y_sb"))
            z_t.append(rows.tile([P, FEATURE_BLOCKS, P], F32, name="z_t"))
            result.append(rows.tile([P, N], F32, name="result"))
            squares.append(rows.tile([P, N], BF16, name="squares"))
            row_sum.append(small.tile([P, BANKS], F32, name="row_sum"))
            mean_junk.append(small.tile([P, BANKS], F32, name="mean_junk"))
            neg_mean.append(small.tile([P, 1], F32, name="neg_mean"))
            sum_squares.append(small.tile([P, 1], F32, name="sum_squares"))
            rstd.append(small.tile([P, 1], F32, name="rstd"))
        bank_of = {}

        nc.vector.memset(ones[:], 1.0)
        nc.vector.memset(eps[:], EPS)
        nc.vector.memset(w_scales[:].rearrange("p g n -> p (g n)").bitcast(I32), 0)
        nc.vector.memset(b_row[:].bitcast(I32), 0)
        nc.vector.memset(gain_shift_rows[:].bitcast(I32), 0)
        make_identity(nc, identity[:])
        make_identity(nc, identity_bf[:])

        nc.sync.dma_start(out=h_sb[0][:], in_=h_tiles[0])
        nc.scalar.activation(out=table_warm[:], in_=eps[:], func=ACT.Abs_reciprocal_sqrt)
        nc.sync.dma_start(
            out=w_words[0][:].bitcast(I32),
            in_=attn_out_W_words.rearrange("g p b -> p g b")[:, :, 0 * 2 * BANK : 1 * 2 * BANK].bitcast(I32),
        )
        for q in range(4):
            nc.sync.dma_start(
                out=w_scales[32 * q : 32 * q + 4, :, :].bitcast(I32),
                in_=attn_out_W_scales[:, 4 * q : 4 * q + 4, :].rearrange("g r n -> r g n").bitcast(I32),
            )
        nc.sync.dma_start(out=b_row[0:1, :], in_=attn_out_b.unsqueeze(0))
        nc.sync.dma_start(out=h_sb[1][:], in_=h_tiles[1])
        nc.sync.dma_start(
            out=w_words[1][:].bitcast(I32),
            in_=attn_out_W_words.rearrange("g p b -> p g b")[:, :, 1 * 2 * BANK : 2 * 2 * BANK].bitcast(I32),
        )
        nc.sync.dma_start(out=h_sb[2][:], in_=h_tiles[2])
        nc.sync.dma_start(out=h_sb[3][:], in_=h_tiles[3])
        nc.sync.dma_start(
            out=gain_shift_rows[0:FEATURE_BLOCKS, :], in_=attn_norm_g.rearrange("(f p) -> f p", p=P)
        )
        nc.sync.dma_start(
            out=gain_shift_rows[FEATURE_BLOCKS : 2 * FEATURE_BLOCKS, :],
            in_=attn_norm_b.rearrange("(f p) -> f p", p=P),
        )
        nc.sync.dma_start(out=x_sb[:], in_=x.flatten_outer_dims().rearrange("(i p) n -> p i n", p=P))

        clock_bank = psum_clock.tile([P, BANK], F32)

        def clock():
            for r in range(CLOCK_WARM_MATMULS):
                nc.tensor.matmul(out=clock_bank[:], lhsT=ones[:], rhs=ones[:].unsqueeze(1).to_broadcast([P, BLOCKS_PER_BANK, P]), start=True, stop=True)

        def mxk(n=2):
            for r in range(n):
                nc.tensor.matmul(out=clock_bank[:, 0:P], lhsT=identity[:], rhs=identity[:], start=True, stop=True)

        def spread():
            b_bank = psum.tile([P, N], BF16, tag="bank")
            for j in range(BANKS):
                cols = slice(j * BANK, (j + 1) * BANK)
                nc.tensor.matmul(out=b_bank[:, cols], lhsT=ones[:], rhs=b_row[:, cols], start=True, stop=True)
            bank_of["b"] = b_bank

        def ball(engine="V"):
            if engine == "V":
                nc.vector.tensor_copy(out=b_all[:], in_=bank_of["b"][:])
            else:
                nc.scalar.copy(out=b_all[:], in_=bank_of["b"][:])

        def gsT():
            flipped = psum.tile([P, P], BF16, tag="bank")
            nc.tensor.transpose(out=flipped[:], in_=gain_shift_rows[:], identity=identity_bf[:])
            bank_of["gs"] = flipped

        def gscp():
            nc.scalar.copy(out=gain_shift[:], in_=bank_of["gs"][:, 0 : 2 * FEATURE_BLOCKS])

        def flipT(i):
            h_words = h_sb[i][:].bitcast(F32)
            flipped = psum.tile([P, PASSES, 2, P], F32, tag="bank")
            for g in range(PASSES):
                for u in range(2):
                    nc.tensor.transpose(
                        out=flipped[:, g, u, :],
                        in_=h_words[:, g * WORDS + u : (g + 1) * WORDS : 2],
                        identity=identity[:],
                    )
            bank_of[("f", i)] = flipped

        def flipTg(i, g):
            h_words = h_sb[i][:].bitcast(F32)
            flipped = psum.tile([P, 2, P], F32, tag="bank")
            for u in range(2):
                nc.tensor.transpose(
                    out=flipped[:, u, :],
                    in_=h_words[:, g * WORDS + u : (g + 1) * WORDS : 2],
                    identity=identity[:],
                )
            bank_of[("f", i, g)] = flipped

        def cpg(i, g):
            nc.scalar.copy(
                out=grouped[i][:, g * K_PASS : (g + 1) * K_PASS].bitcast(F32).rearrange("p (r u) -> p r u", u=2),
                in_=bank_of[("f", i, g)][:].rearrange("p u r -> p r u"),
            )

        def qg(i, g):
            nc.vector.quantize_mx(
                out=h_codes[:, i, g * P : (g + 1) * P].bitcast(FP8X4),
                scales=h_scales[:, i, g * P : (g + 1) * P],
                in_=grouped[i][:, g * K_PASS : (g + 1) * K_PASS],
            )

        def mxg(i, j, g):
            if g == 0:
                acc = psum.tile([P, BANK], F32, tag="bank")
                bank_of[("a", i, j)] = acc
            nc.tensor.matmul_mx(
                out=bank_of[("a", i, j)][:],
                lhsT=h_codes[:, i, g * P : (g + 1) * P].bitcast(FP8X4),
                lhsT_scale=h_scales[:, i, g * P : (g + 1) * P],
                rhs=w_words[j][:, g, :].bitcast(FP4X4),
                rhs_scale=w_scales[:, g, j * BANK : (j + 1) * BANK],
                start=(g == 0),
                stop=(g == PASSES - 1),
            )

        def cp(i):
            nc.scalar.copy(
                out=grouped[i][:].bitcast(F32).rearrange("p (g r u) -> p g r u", g=PASSES, u=2),
                in_=bank_of[("f", i)][:].rearrange("p g u r -> p g r u"),
            )

        def q(i):
            nc.vector.quantize_mx(
                out=h_codes[:, i, :].bitcast(FP8X4), scales=h_scales[:, i, :], in_=grouped[i][:]
            )

        def mxj(i, j):
            acc = psum.tile([P, BANK], F32, tag="bank")
            for g in range(PASSES):
                nc.tensor.matmul_mx(
                    out=acc[:],
                    lhsT=h_codes[:, i, g * P : (g + 1) * P].bitcast(FP8X4),
                    lhsT_scale=h_scales[:, i, g * P : (g + 1) * P],
                    rhs=w_words[j][:, g, :].bitcast(FP4X4),
                    rhs_scale=w_scales[:, g, j * BANK : (j + 1) * BANK],
                    start=(g == 0),
                    stop=(g == PASSES - 1),
                )
            bank_of[("a", i, j)] = acc

        def v1j(i, j):
            cols = slice(j * BANK, (j + 1) * BANK)
            nc.vector.scalar_tensor_tensor(
                out=o_sb[i][:, cols],
                in0=bank_of[("a", i, j)][:],
                scalar=1.0,
                in1=b_all[:, cols],
                op0=ALU.mult,
                op1=ALU.add,
                accum_out=row_sum[i][:, j : j + 1],
            )

        def nm(i, engine="S"):
            if engine == "S":
                nc.scalar.activation(
                    out=mean_junk[i][:], in_=row_sum[i][:], func=ACT.Identity, scale=-1.0 / N, accum_out=neg_mean[i][:]
                )
            else:
                nc.vector.tensor_scalar(
                    out=mean_junk[i][:], in0=row_sum[i][:], scalar1=-1.0 / N, scalar2=None,
                    op0=ALU.mult, op1=ALU.add, accum_out=neg_mean[i][:],
                )

        def dev(i):
            nc.scalar.activation(
                out=squares[i][:], in_=o_sb[i][:], func=ACT.Square, bias=neg_mean[i][:], accum_out=sum_squares[i][:]
            )

        def rs(i):
            nc.scalar.activation(
                out=rstd[i][:], in_=sum_squares[i][:], func=ACT.Abs_reciprocal_sqrt, scale=1.0 / N, bias=eps[:]
            )

        def yj(i, j, engine="V"):
            cols = slice(j * BANK, (j + 1) * BANK)
            if engine == "V":
                nc.vector.tensor_scalar(
                    out=y_sb[i][:, cols], in0=o_sb[i][:, cols], scalar1=neg_mean[i][:], scalar2=rstd[i][:],
                    op0=ALU.add, op1=ALU.mult,
                )
                return
            nc.gpsimd.tensor_scalar(
                out=y_sb[i][:, cols], in0=o_sb[i][:, cols], scalar1=neg_mean[i][:], scalar2=rstd[i][:],
                op0=ALU.add, op1=ALU.mult,
            )

        def fwd(i, j):
            y_t = psum.tile([P, BLOCKS_PER_BANK, P], F32, tag="bank")
            for m in range(BLOCKS_PER_BANK):
                f = j * BLOCKS_PER_BANK + m
                nc.tensor.transpose(out=y_t[:, m, :], in_=y_sb[i][:, f * P : (f + 1) * P], identity=identity[:])
            bank_of[("y", i, j)] = y_t

        def zt(i, j, engine="S"):
            y_t = bank_of[("y", i, j)]
            for m in range(BLOCKS_PER_BANK):
                f = j * BLOCKS_PER_BANK + m
                gain = gain_shift[:, f : f + 1]
                shift = gain_shift[:, FEATURE_BLOCKS + f : FEATURE_BLOCKS + f + 1]
                if engine == "V":
                    nc.vector.tensor_scalar(
                        out=z_t[i][:, f, :], in0=y_t[:, m, :], scalar1=gain, scalar2=shift, op0=ALU.mult, op1=ALU.add
                    )
                else:
                    nc.scalar.activation(out=z_t[i][:, f, :], in_=y_t[:, m, :], func=ACT.Identity, scale=gain, bias=shift)

        def back(i, j):
            z = psum.tile([P, BANK], F32, tag="bank")
            for m in range(BLOCKS_PER_BANK):
                nc.tensor.transpose(
                    out=z[:, m * P : (m + 1) * P], in_=z_t[i][:, j * BLOCKS_PER_BANK + m, :], identity=identity[:]
                )
            bank_of[("z", i, j)] = z

        def add(i, j):
            cols = slice(j * BANK, (j + 1) * BANK)
            nc.vector.tensor_tensor(out=result[i][:, cols], in0=bank_of[("z", i, j)][:], in1=x_sb[:, i, cols], op=ALU.add)
            nc.sync.dma_start(out=out_tiles[i][:, cols], in_=result[i][:, cols])

        clock()
        flipTg(0, 0)
        cpg(0, 0)
        flipTg(0, 1)
        cpg(0, 1)
        spread()
        qg(0, 0)
        qg(0, 1)
        ball()
        flipT(1)
        cp(1)
        mxg(0, 0, 0)
        mxg(0, 0, 1)
        mxg(0, 1, 0)
        mxg(0, 1, 1)
        v1j(0, 0)
        q(1)
        v1j(0, 1)
        flipT(2)
        cp(2)
        flipT(3)
        cp(3)
        gsT()
        gscp()
        mxj(1, 0)
        mxj(1, 1)
        q(2)
        nm(0, "V")
        dev(0)
        rs(0)
        v1j(1, 0)
        v1j(1, 1)
        q(3)
        nm(1, "V")
        mxj(2, 0)
        mxj(2, 1)
        mxj(3, 0)
        mxj(3, 1)
        yj(0, 0, "G")
        yj(0, 1, "G")
        v1j(2, 0)
        dev(1)
        rs(1)
        v1j(2, 1)
        nm(2, "V")
        yj(1, 0, "G")
        yj(1, 1, "G")
        fwd(0, 0)
        fwd(0, 1)
        mxk()
        v1j(3, 0)
        dev(2)
        rs(2)
        v1j(3, 1)
        nm(3, "V")
        yj(2, 0, "G")
        yj(2, 1, "G")
        dev(3)
        rs(3)
        zt(0, 0, "V")
        zt(0, 1, "V")
        fwd(1, 0)
        back(0, 0)
        mxk()
        fwd(1, 1)
        back(0, 1)
        zt(1, 0, "V")
        zt(1, 1)
        add(0, 0)
        yj(3, 0)
        yj(3, 1)
        add(0, 1)
        fwd(2, 0)
        back(1, 0)
        fwd(2, 1)
        zt(2, 0)
        zt(2, 1)
        back(1, 1)
        add(1, 0)
        fwd(3, 0)
        fwd(3, 1)
        add(1, 1)
        back(2, 0)
        back(2, 1)
        zt(3, 0)
        zt(3, 1)
        add(2, 0)
        add(2, 1)
        back(3, 0)
        back(3, 1)
        add(3, 0)
        add(3, 1)
